import numpy as np
import ml_dtypes


def mxq(x, axis, fmt="e4m3"):
    dtype, down = {"e4m3": (ml_dtypes.float8_e4m3fn, 7), "e5m2": (ml_dtypes.float8_e5m2, 14)}[fmt]
    v = np.moveaxis(np.asarray(x, np.float32).astype(ml_dtypes.bfloat16).astype(np.float64), axis, -1)
    blocks = v.reshape(v.shape[:-1] + (-1, 32))
    amax = np.abs(blocks).max(-1, keepdims=True)
    byte = np.maximum(np.where(amax > 0, np.frexp(amax)[1] - 1 + 127, 0) - down, 1)
    scale = np.exp2(byte - 127.0)
    codes = (blocks / scale).astype(np.float32).astype(dtype).astype(np.float64)
    return np.moveaxis((codes * scale).reshape(v.shape), -1, axis)


WIDE = False


def mx_kscale(k):
    if not WIDE:
        return np.ones(k)
    levels = np.array([10, -10, 5, -5, 0])
    a = np.random.permutation(np.resize(levels, k // 512 * 4)).reshape(k // 512, 4)
    idx = np.arange(k)
    return np.exp2(a[idx // 512, idx % 128 // 32])


BF16 = ml_dtypes.bfloat16


def bf(x):
    return np.asarray(x, np.float32).astype(BF16)


def f64(x):
    return np.asarray(x).astype(np.float64)


B, C, S, OUT = 8192, 4, 16, 512
IN = C * S * S
HS = S // 2
SUB, BLK = 4, 32


def haar_dwt2_features(x):
    x4 = x.reshape(x.shape[0], C, S, S)
    a = x4[:, :, 0::2, 0::2]
    bq = x4[:, :, 0::2, 1::2]
    c = x4[:, :, 1::2, 0::2]
    d = x4[:, :, 1::2, 1::2]
    LL = (a + bq + c + d) * 0.5
    LH = (a + bq - c - d) * 0.5
    HL = (a - bq + c - d) * 0.5
    HH = (a - bq - c + d) * 0.5
    t = np.stack([LL, LH, HL, HH], axis=2)
    return t.reshape(x.shape[0], -1)


def setup_inputs():
    u = np.unique(mx_kscale(IN))
    p = np.stack([u[::-1], u], axis=1).reshape(-1)[:u.size]
    g = np.repeat(np.resize(p, IN // SUB // BLK), BLK).reshape(C, HS, HS)
    gx = np.repeat(np.repeat(g, 2, axis=1), 2, axis=2).reshape(IN)
    gt = np.repeat(g[:, None], SUB, axis=1).reshape(IN)
    return {"x": bf(np.random.standard_normal((B, IN)) * gx),
            "W": bf(np.random.standard_normal((OUT, IN)) * (1.0 / np.sqrt(IN)) / gt),
            "b": bf(np.random.standard_normal(OUT) * 0.5)}


def reference(x, W, b):
    t = haar_dwt2_features(f64(x))
    return (mxq(t, 1, "e4m3") @ mxq(f64(W), 1, "e4m3").T) + f64(b)

@@ -1,0 +1,182 @@
+from contextlib import ExitStack
+
+import concourse.bass as bass
+import concourse.mybir as mybir
+import concourse.tile as tile
+from concourse.masks import make_identity
+
+FP8X4 = mybir.dt.float8_e4m3fn_x4
+BF16 = mybir.dt.bfloat16
+F32 = mybir.dt.float32
+U32 = mybir.dt.uint32
+U8 = mybir.dt.uint8
+ALU = mybir.AluOpType
+ACT = mybir.ActivationFunctionType
+
+FLOPS = 2 * 8192 * 1024 * 512
+
+P = 128
+T = 4
+ROWS = P * T
+FEAT = 1024
+OUT = 512
+GROUPS = 8192 // ROWS
+KINDS = "VPVVPVPVVPVVPVPV"
+
+
+def tile_waveletlinearlayer_t_kernel(tc, x, W, b, out):
+    nc = tc.nc
+    with ExitStack() as ctx:
+        const = ctx.enter_context(tc.tile_pool(name="const", bufs=1))
+        xin = ctx.enter_context(tc.tile_pool(name="xin", bufs=4))
+        upool = ctx.enter_context(tc.tile_pool(name="upool", bufs=2))
+        tpool = ctx.enter_context(tc.tile_pool(name="tpool", bufs=3))
+        xtpool = ctx.enter_context(tc.tile_pool(name="xtpool", bufs=3))
+        gpool = ctx.enter_context(tc.tile_pool(name="gpool", bufs=2))
+        cpool = ctx.enter_context(tc.tile_pool(name="cpool", bufs=2))
+        opool = ctx.enter_context(tc.tile_pool(name="opool", bufs=3))
+        ps_t = ctx.enter_context(tc.psum_pool(name="ps_t", bufs=3))
+        ps_h = ctx.enter_context(tc.psum_pool(name="ps_h", bufs=2))
+        ps_a = ctx.enter_context(tc.psum_pool(name="ps_a", bufs=3))
+
+        def load_x(gi):
+            x_sb = xin.tile([P, T * FEAT], BF16)
+            nc.sync.dma_start(
+                out=x_sb[:],
+                in_=x[gi * ROWS : (gi + 1) * ROWS, :].rearrange("(p t) k -> p (t k)", t=T),
+            )
+            return x_sb
+
+        x_tiles = [None] * GROUPS
+        x_tiles[0] = load_x(0)
+
+        w_sb = const.tile([P, 4, FEAT], BF16)
+        nc.sync.dma_start(out=w_sb[:], in_=W.rearrange("(a p) k -> p a k", p=P))
+        bias = const.tile([P, OUT], BF16)
+        nc.sync.dma_start(out=bias[:], in_=b.partition_broadcast(P))
+
+        ident = const.tile([P, P], BF16)
+        make_identity(nc, ident[:])
+
+        h_a = const.tile([P, P], F32)
+        iv = ident[:].rearrange("p (q h s c) -> p s q h c", q=2, h=2, s=2, c=16)
+        av = h_a[:].rearrange("p (q v h c) -> p v q h c", q=2, v=2, h=2, c=16)
+        nc.vector.tensor_tensor(out=av[:, 0], in0=iv[:, 0], in1=iv[:, 1], op=ALU.add)
+        nc.vector.tensor_tensor(out=av[:, 1], in0=iv[:, 0], in1=iv[:, 1], op=ALU.subtract)
+        h_b = const.tile([P, P], F32)
+        ae = h_a[:].rearrange("p (w r e) -> p e w r", r=32, e=2)
+        hv = h_b[:].rearrange("p (w h r) -> p h w r", h=2, r=32)
+        nc.vector.tensor_tensor(out=hv[:, 0], in0=ae[:, 0], in1=ae[:, 1], op=ALU.add)
+        nc.vector.tensor_tensor(out=hv[:, 1], in0=ae[:, 0], in1=ae[:, 1], op=ALU.subtract)
+        haar = const.tile([P, P], BF16)
+        nc.vector.tensor_scalar_mul(out=haar[:], in0=h_b[:], scalar1=0.5)
+
+        def transposes(src, tau):
+            xt = ps_t.tile([P, 2 * 4 * P], BF16)
+            for g in range(2):
+                for t in range(4):
+                    c0 = t * (T * 256) + tau * 256 + g * P
+                    nc.tensor.transpose(
+                        xt[:, (g * 4 + t) * P : (g * 4 + t + 1) * P], src[:, c0 : c0 + P], ident[:]
+                    )
+            return xt
+
+        def quantise(grouped, codes, scales):
+            for g in range(2):
+                nc.vector.quantize_mx(
+                    out=codes[:, g, :].bitcast(FP8X4), scales=scales[:, g, :], in_=grouped[:, g, :]
+                )
+
+        def back_direct(src, scale, grouped):
+            for tau in range(T):
+                xt = transposes(src, tau)
+                nc.scalar.activation(
+                    out=grouped[:, :, tau * 512 : (tau + 1) * 512].rearrange(
+                        "p g (n t) -> p g n t", t=4
+                    ),
+                    in_=xt[:].rearrange("p (g t n) -> p g n t", g=2, t=4),
+                    func=ACT.Copy,
+                    scale=scale,
+                )
+
+        w_pm = const.tile([P, 4 * FEAT], BF16)
+        wv = w_pm[:].rearrange("p (t a m j) -> p a t m j", t=4, a=4, m=32, j=8)
+        for a in range(4):
+            nc.scalar.copy(
+                out=wv[:, a], in_=w_sb[:, a, :].rearrange("p (m t j) -> p t m j", m=32, t=4, j=8)
+            )
+        w_grouped = const.tile([P, 2, 4 * OUT], BF16, align_bytes=64)
+        w_codes = const.tile([P, 2, OUT], U32, align_bytes=64)
+        w_scales = const.tile([P, 2, OUT], U8, align_bytes=64)
+        back_direct(w_pm, 1.0, w_grouped)
+        quantise(w_grouped, w_codes, w_scales)
+
+        for gi in range(GROUPS):
+            for nxt in range(gi + 1, min(gi + 3, GROUPS)):
+                if x_tiles[nxt] is None:
+                    x_tiles[nxt] = load_x(nxt)
+            x_sb = x_tiles[gi]
+            grouped = gpool.tile([P, 2, T * 512], BF16, align_bytes=64)
+            codes = cpool.tile([P, 2, T * P], U32, align_bytes=64)
+            scales = cpool.tile([P, 2, T * P], U8, align_bytes=64)
+
+            if KINDS[gi] == "V":
+                u = upool.tile([P, T * FEAT], F32)
+                xv = x_sb[:].rearrange(
+                    "p (q h t s c) -> p s t q h c", q=4 * T, h=2, t=4, s=2, c=16
+                )
+                uv = u[:].rearrange("p (t q v h c) -> p v t q h c", t=4, q=4 * T, v=2, h=2, c=16)
+                nc.vector.tensor_tensor(out=uv[:, 0], in0=xv[:, 0], in1=xv[:, 1], op=ALU.add)
+                nc.vector.tensor_tensor(out=uv[:, 1], in0=xv[:, 0], in1=xv[:, 1], op=ALU.subtract)
+                tp = tpool.tile([P, T * FEAT], BF16)
+                ue = u[:].rearrange("p (w r e) -> p e w r", r=32, e=2)
+                tv = tp[:].rearrange("p (w h r) -> p h w r", h=2, r=32)
+                nc.vector.tensor_tensor(out=tv[:, 0], in0=ue[:, 0], in1=ue[:, 1], op=ALU.add)
+                nc.vector.tensor_tensor(out=tv[:, 1], in0=ue[:, 0], in1=ue[:, 1], op=ALU.subtract)
+                back_direct(tp, 0.5, grouped)
+            else:
+                xp = tpool.tile([P, T * FEAT // 2], F32, tag="tp")
+                nc.scalar.copy(
+                    out=xp[:].rearrange("p (t m c) -> p t m c", t=4, m=8 * T, c=16),
+                    in_=x_sb[:].bitcast(F32).rearrange("p (m t c) -> p t m c", m=8 * T, t=4, c=16),
+                )
+                xpb = xp[:].bitcast(BF16)
+                for tau in range(T):
+                    xt = transposes(xpb, tau)
+                    x_t = xtpool.tile([P, 2 * 4 * P], BF16)
+                    nc.scalar.copy(out=x_t[:], in_=xt[:])
+                    for g in range(2):
+                        hp = ps_h.tile([P, 512], F32)
+                        nc.tensor.matmul(
+                            out=hp[:],
+                            lhsT=haar[:],
+                            rhs=x_t[:, g * 512 : (g + 1) * 512],
+                            start=True,
+                            stop=True,
+                        )
+                        nc.scalar.copy(
+                            out=grouped[:, g, tau * 512 : (tau + 1) * 512].rearrange(
+                                "p (n t) -> p n t", t=4
+                            ),
+                            in_=hp[:].rearrange("p (t n) -> p n t", t=4),
+                        )
+            quantise(grouped, codes, scales)
+
+            o_sb = opool.tile([P, T, OUT], F32)
+            for tau in range(T):
+                acc = ps_a.tile([P, OUT], F32)
+                for g in range(2):
+                    nc.tensor.matmul_mx(
+                        out=acc[:],
+                        lhsT=codes[:, g, tau * P : (tau + 1) * P].bitcast(FP8X4),
+                        lhsT_scale=scales[:, g, tau * P : (tau + 1) * P],
+                        rhs=w_codes[:, g, :].bitcast(FP8X4),
+                        rhs_scale=w_scales[:, g, :],
+                        start=(g == 0),
+                        stop=(g == 1),
+                    )
+                nc.vector.tensor_tensor(out=o_sb[:, tau, :], in0=acc[:], in1=bias[:], op=ALU.add)
+            nc.sync.dma_start(
+                out=out[gi * ROWS : (gi + 1) * ROWS, :].rearrange("(p t) o -> p t o", t=T),
+                in_=o_sb[:],
+            )

@@ -1,8 +1,6 @@
 from contextlib import ExitStack
 
-import concourse.bass as bass
 import concourse.mybir as mybir
-import concourse.tile as tile
 from concourse.masks import make_identity
 
 FP8X4 = mybir.dt.float8_e4m3fn_x4
@@ -21,7 +19,8 @@ ROWS = P * T
 FEAT = 1024
 OUT = 512
 GROUPS = 8192 // ROWS
-KINDS = "VPVVPVPVVPVVPVPV"
+KINDS = "GPGGPGPGGPGGPGPG"
+ON_VECTOR = [0] * GROUPS
 
 
 def tile_waveletlinearlayer_t_kernel(tc, x, W, b, out):
@@ -30,14 +29,14 @@ def tile_waveletlinearlayer_t_kernel(tc, x, W, b, out):
         const = ctx.enter_context(tc.tile_pool(name="const", bufs=1))
         xin = ctx.enter_context(tc.tile_pool(name="xin", bufs=4))
         upool = ctx.enter_context(tc.tile_pool(name="upool", bufs=2))
-        tpool = ctx.enter_context(tc.tile_pool(name="tpool", bufs=3))
+        tpool = ctx.enter_context(tc.tile_pool(name="tpool", bufs=2))
         xtpool = ctx.enter_context(tc.tile_pool(name="xtpool", bufs=3))
-        gpool = ctx.enter_context(tc.tile_pool(name="gpool", bufs=2))
-        cpool = ctx.enter_context(tc.tile_pool(name="cpool", bufs=2))
+        epool = ctx.enter_context(tc.tile_pool(name="epool", bufs=3))
+        gpool = ctx.enter_context(tc.tile_pool(name="gpool", bufs=3))
+        cpool = ctx.enter_context(tc.tile_pool(name="cpool", bufs=3))
         opool = ctx.enter_context(tc.tile_pool(name="opool", bufs=3))
-        ps_t = ctx.enter_context(tc.psum_pool(name="ps_t", bufs=3))
-        ps_h = ctx.enter_context(tc.psum_pool(name="ps_h", bufs=2))
-        ps_a = ctx.enter_context(tc.psum_pool(name="ps_a", bufs=3))
+        ps_w = ctx.enter_context(tc.psum_pool(name="ps_w", bufs=6))
+        ps_a = ctx.enter_context(tc.psum_pool(name="ps_a", bufs=2))
 
         def load_x(gi):
             x_sb = xin.tile([P, T * FEAT], BF16)
@@ -52,27 +51,17 @@ def tile_waveletlinearlayer_t_kernel(tc, x, W, b, out):
 
         w_sb = const.tile([P, 4, FEAT], BF16)
         nc.sync.dma_start(out=w_sb[:], in_=W.rearrange("(a p) k -> p a k", p=P))
+        x_tiles[1] = load_x(1)
         bias = const.tile([P, OUT], BF16)
         nc.sync.dma_start(out=bias[:], in_=b.partition_broadcast(P))
 
         ident = const.tile([P, P], BF16)
         make_identity(nc, ident[:])
-
-        h_a = const.tile([P, P], F32)
-        iv = ident[:].rearrange("p (q h s c) -> p s q h c", q=2, h=2, s=2, c=16)
-        av = h_a[:].rearrange("p (q v h c) -> p v q h c", q=2, v=2, h=2, c=16)
-        nc.vector.tensor_tensor(out=av[:, 0], in0=iv[:, 0], in1=iv[:, 1], op=ALU.add)
-        nc.vector.tensor_tensor(out=av[:, 1], in0=iv[:, 0], in1=iv[:, 1], op=ALU.subtract)
-        h_b = const.tile([P, P], F32)
-        ae = h_a[:].rearrange("p (w r e) -> p e w r", r=32, e=2)
-        hv = h_b[:].rearrange("p (w h r) -> p h w r", h=2, r=32)
-        nc.vector.tensor_tensor(out=hv[:, 0], in0=ae[:, 0], in1=ae[:, 1], op=ALU.add)
-        nc.vector.tensor_tensor(out=hv[:, 1], in0=ae[:, 0], in1=ae[:, 1], op=ALU.subtract)
-        haar = const.tile([P, P], BF16)
-        nc.vector.tensor_scalar_mul(out=haar[:], in0=h_b[:], scalar1=0.5)
+        ident_f = const.tile([P, P], F32)
+        make_identity(nc, ident_f[:])
 
         def transposes(src, tau):
-            xt = ps_t.tile([P, 2 * 4 * P], BF16)
+            xt = ps_w.tile([P, 2 * 4 * P], BF16, tag="w")
             for g in range(2):
                 for t in range(4):
                     c0 = t * (T * 256) + tau * 256 + g * P
@@ -87,66 +76,118 @@ def tile_waveletlinearlayer_t_kernel(tc, x, W, b, out):
                     out=codes[:, g, :].bitcast(FP8X4), scales=scales[:, g, :], in_=grouped[:, g, :]
                 )
 
-        def back_direct(src, scale, grouped):
-            for tau in range(T):
-                xt = transposes(src, tau)
-                nc.scalar.activation(
-                    out=grouped[:, :, tau * 512 : (tau + 1) * 512].rearrange(
+        def w_set(w_pm, name):
+            w_grouped = const.tile([P, 2, 4 * OUT], BF16, align_bytes=64, name="wg" + name)
+            w_codes = const.tile([P, 2, OUT], U32, align_bytes=64, name="wc" + name)
+            w_scales = const.tile([P, 2, OUT], U8, align_bytes=64, name="ws" + name)
+            for a in range(4):
+                xt = transposes(w_pm, a)
+                nc.vector.tensor_copy(
+                    out=w_grouped[:, :, a * 512 : (a + 1) * 512].rearrange(
                         "p g (n t) -> p g n t", t=4
                     ),
                     in_=xt[:].rearrange("p (g t n) -> p g n t", g=2, t=4),
-                    func=ACT.Copy,
-                    scale=scale,
                 )
+            quantise(w_grouped, w_codes, w_scales)
+            return w_codes, w_scales
 
-        w_pm = const.tile([P, 4 * FEAT], BF16)
-        wv = w_pm[:].rearrange("p (t a m j) -> p a t m j", t=4, a=4, m=32, j=8)
-        for a in range(4):
-            nc.scalar.copy(
-                out=wv[:, a], in_=w_sb[:, a, :].rearrange("p (m t j) -> p t m j", m=32, t=4, j=8)
-            )
-        w_grouped = const.tile([P, 2, 4 * OUT], BF16, align_bytes=64)
-        w_codes = const.tile([P, 2, OUT], U32, align_bytes=64)
-        w_scales = const.tile([P, 2, OUT], U8, align_bytes=64)
-        back_direct(w_pm, 1.0, w_grouped)
-        quantise(w_grouped, w_codes, w_scales)
+        w_pm5 = const.tile([P, 4 * FEAT], BF16)
+        w5o = w_pm5[:].rearrange(
+            "p (t a h c r j) -> p t h a c r j", t=4, a=4, h=2, c=4, r=4, j=8
+        )
+        w5i = w_sb[:].rearrange("p a (c h r t j) -> p t h a c r j", c=4, h=2, r=4, t=4, j=8)
+        for t in range(4):
+            for h in range(2):
+                nc.scalar.copy(out=w5o[:, t, h], in_=w5i[:, t, h])
+        wc5, ws5 = w_set(w_pm5, "5")
 
-        for gi in range(GROUPS):
-            for nxt in range(gi + 1, min(gi + 3, GROUPS)):
-                if x_tiles[nxt] is None:
-                    x_tiles[nxt] = load_x(nxt)
+        w_pm4 = const.tile([P, 4 * FEAT], BF16)
+        w4o = w_pm4[:].rearrange("p (t a m j) -> p t a m j", t=4, a=4, m=32, j=8)
+        w4i = w_sb[:].rearrange("p a (m t j) -> p t a m j", m=32, t=4, j=8)
+        for t in range(4):
+            nc.scalar.copy(out=w4o[:, t], in_=w4i[:, t])
+        wc4, ws4 = w_set(w_pm4, "4")
+
+        h_a = const.tile([P, P], F32)
+        iv = ident[:].rearrange("p (q h s c) -> p s q h c", q=2, h=2, s=2, c=16)
+        av = h_a[:].rearrange("p (q v h c) -> p v q h c", q=2, v=2, h=2, c=16)
+        nc.vector.tensor_tensor(out=av[:, 0], in0=iv[:, 0], in1=iv[:, 1], op=ALU.add)
+        nc.vector.tensor_tensor(out=av[:, 1], in0=iv[:, 0], in1=iv[:, 1], op=ALU.subtract)
+        h_b = const.tile([P, P], F32)
+        ae = h_a[:].rearrange("p (w r e) -> p e w r", r=32, e=2)
+        hv = h_b[:].rearrange("p (w h r) -> p h w r", h=2, r=32)
+        nc.vector.tensor_tensor(out=hv[:, 0], in0=ae[:, 0], in1=ae[:, 1], op=ALU.add)
+        nc.vector.tensor_tensor(out=hv[:, 1], in0=ae[:, 0], in1=ae[:, 1], op=ALU.subtract)
+        haar = const.tile([P, P], BF16)
+        nc.vector.tensor_scalar_mul(out=haar[:], in0=h_b[:], scalar1=0.5)
+
+        def front(gi):
             x_sb = x_tiles[gi]
-            grouped = gpool.tile([P, 2, T * 512], BF16, align_bytes=64)
-            codes = cpool.tile([P, 2, T * P], U32, align_bytes=64)
-            scales = cpool.tile([P, 2, T * P], U8, align_bytes=64)
-
-            if KINDS[gi] == "V":
+            if KINDS[gi] == "G":
                 u = upool.tile([P, T * FEAT], F32)
-                xv = x_sb[:].rearrange(
-                    "p (q h t s c) -> p s t q h c", q=4 * T, h=2, t=4, s=2, c=16
+                xg = x_sb[:].rearrange(
+                    "p (q h t s j e) -> p s e t q h j", q=4 * T, h=2, t=4, s=2, j=8, e=2
                 )
-                uv = u[:].rearrange("p (t q v h c) -> p v t q h c", t=4, q=4 * T, v=2, h=2, c=16)
-                nc.vector.tensor_tensor(out=uv[:, 0], in0=xv[:, 0], in1=xv[:, 1], op=ALU.add)
-                nc.vector.tensor_tensor(out=uv[:, 1], in0=xv[:, 0], in1=xv[:, 1], op=ALU.subtract)
-                tp = tpool.tile([P, T * FEAT], BF16)
-                ue = u[:].rearrange("p (w r e) -> p e w r", r=32, e=2)
-                tv = tp[:].rearrange("p (w h r) -> p h w r", h=2, r=32)
-                nc.vector.tensor_tensor(out=tv[:, 0], in0=ue[:, 0], in1=ue[:, 1], op=ALU.add)
-                nc.vector.tensor_tensor(out=tv[:, 1], in0=ue[:, 0], in1=ue[:, 1], op=ALU.subtract)
-                back_direct(tp, 0.5, grouped)
+                uv = u[:].rearrange(
+                    "p (e t q v h j) -> p e v t q h j", e=2, t=4, q=4 * T, v=2, h=2, j=8
+                )
+                k = 0
+                for e in range(2):
+                    for v in range(2):
+                        eng = nc.vector if k < ON_VECTOR[gi] else nc.gpsimd
+                        eng.tensor_tensor(
+                            out=uv[:, e, v],
+                            in0=xg[:, 0, e],
+                            in1=xg[:, 1, e],
+                            op=(ALU.add if v == 0 else ALU.subtract),
+                        )
+                        k += 1
+                return u
+            xp = tpool.tile([P, T * FEAT // 2], F32)
+            nc.scalar.copy(
+                out=xp[:].rearrange("p (t m c) -> p t m c", t=4, m=8 * T, c=16),
+                in_=x_sb[:].bitcast(F32).rearrange("p (m t c) -> p t m c", m=8 * T, t=4, c=16),
+            )
+            return xp
+
+        def middle(gi, fr, grouped):
+            if KINDS[gi] == "G":
+                for tau in range(T):
+                    banks = []
+                    for e in range(2):
+                        bank = ps_w.tile([P, 512], F32, tag="w", name="bank")
+                        for t in range(4):
+                            c0 = e * (T * 512) + t * (T * P) + tau * P
+                            nc.tensor.transpose(
+                                bank[:, t * P : (t + 1) * P], fr[:, c0 : c0 + P], ident_f[:]
+                            )
+                        banks.append(bank)
+                    e1h = epool.tile([P, P, 4], F32)
+                    nc.scalar.activation(
+                        out=e1h[:],
+                        in_=banks[1][:].rearrange("p (t n) -> p n t", t=4),
+                        func=ACT.Copy,
+                        scale=0.5,
+                    )
+                    for h in range(2):
+                        nc.vector.scalar_tensor_tensor(
+                            out=grouped[:, h, tau * 512 : (tau + 1) * 512].rearrange(
+                                "p (n t) -> p n t", t=4
+                            ),
+                            in0=banks[0][:].rearrange("p (t n) -> p n t", t=4),
+                            scalar=0.5,
+                            in1=e1h[:],
+                            op0=ALU.mult,
+                            op1=(ALU.add if h == 0 else ALU.subtract),
+                        )
             else:
-                xp = tpool.tile([P, T * FEAT // 2], F32, tag="tp")
-                nc.scalar.copy(
-                    out=xp[:].rearrange("p (t m c) -> p t m c", t=4, m=8 * T, c=16),
-                    in_=x_sb[:].bitcast(F32).rearrange("p (m t c) -> p t m c", m=8 * T, t=4, c=16),
-                )
-                xpb = xp[:].bitcast(BF16)
+                xpb = fr[:].bitcast(BF16)
                 for tau in range(T):
                     xt = transposes(xpb, tau)
                     x_t = xtpool.tile([P, 2 * 4 * P], BF16)
                     nc.scalar.copy(out=x_t[:], in_=xt[:])
                     for g in range(2):
-                        hp = ps_h.tile([P, 512], F32)
+                        hp = ps_w.tile([P, 512], F32, tag="w")
                         nc.tensor.matmul(
                             out=hp[:],
                             lhsT=haar[:],
@@ -160,7 +201,21 @@ def tile_waveletlinearlayer_t_kernel(tc, x, W, b, out):
                             ),
                             in_=hp[:].rearrange("p (t n) -> p n t", t=4),
                         )
+
+        fronts = [None] * GROUPS
+        fronts[0] = front(0)
+        for gi in range(GROUPS):
+            for nxt in range(gi + 1, min(gi + 4, GROUPS)):
+                if x_tiles[nxt] is None:
+                    x_tiles[nxt] = load_x(nxt)
+            if gi + 1 < GROUPS:
+                fronts[gi + 1] = front(gi + 1)
+            grouped = gpool.tile([P, 2, T * 512], BF16, align_bytes=64)
+            codes = cpool.tile([P, 2, T * P], U32, align_bytes=64)
+            scales = cpool.tile([P, 2, T * P], U8, align_bytes=64)
+            middle(gi, fronts[gi], grouped)
             quantise(grouped, codes, scales)
+            w_codes, w_scales = (wc5, ws5) if KINDS[gi] == "G" else (wc4, ws4)
 
             o_sb = opool.tile([P, T, OUT], F32)
             for tau in range(T):

@@ -14,99 +14,237 @@ ACT = mybir.ActivationFunctionType
 FLOPS = 2 * 8192 * 1024 * 512
 
 P = 128
-T = 4
-ROWS = P * T
 FEAT = 1024
 OUT = 512
-GROUPS = 8192 // ROWS
-KINDS = "GPGGPGPGGPGGPGPG"
-ON_VECTOR = [0] * GROUPS
+NG = 5
+NP = 3
+NU = NG + NP
+FRAME = NU * P
+K = 8192 // FRAME
+AHEAD = 3
+PINNED = True
 
 
 def tile_waveletlinearlayer_t_kernel(tc, x, W, b, out):
     nc = tc.nc
     with ExitStack() as ctx:
         const = ctx.enter_context(tc.tile_pool(name="const", bufs=1))
-        xin = ctx.enter_context(tc.tile_pool(name="xin", bufs=4))
+        xgpool = ctx.enter_context(tc.tile_pool(name="xgpool", bufs=3))
+        xppool = ctx.enter_context(tc.tile_pool(name="xppool", bufs=3))
         upool = ctx.enter_context(tc.tile_pool(name="upool", bufs=2))
-        tpool = ctx.enter_context(tc.tile_pool(name="tpool", bufs=2))
-        xtpool = ctx.enter_context(tc.tile_pool(name="xtpool", bufs=3))
-        epool = ctx.enter_context(tc.tile_pool(name="epool", bufs=3))
-        gpool = ctx.enter_context(tc.tile_pool(name="gpool", bufs=3))
-        cpool = ctx.enter_context(tc.tile_pool(name="cpool", bufs=3))
-        opool = ctx.enter_context(tc.tile_pool(name="opool", bufs=3))
-        ps_w = ctx.enter_context(tc.psum_pool(name="ps_w", bufs=6))
-        ps_a = ctx.enter_context(tc.psum_pool(name="ps_a", bufs=2))
+        two = ctx.enter_context(tc.tile_pool(name="two", bufs=2))
+        one = ctx.enter_context(tc.tile_pool(name="one", bufs=1))
+        ps1 = ctx.enter_context(tc.psum_pool(name="ps1", bufs=1))
+        ps2 = ctx.enter_context(tc.psum_pool(name="ps2", bufs=2))
+        if PINNED:
+            ctx.enter_context(tc.manual_schedule())
 
-        def load_x(gi):
-            x_sb = xin.tile([P, T * FEAT], BF16)
+        st = {}
+
+        def frame_rows(ap, k):
+            return ap[k * FRAME : (k + 1) * FRAME, :].rearrange("(p t) f -> p t f", t=NU)
+
+        def load_g(k, cuts):
+            if k >= K:
+                return
+            xg = xgpool.tile([P, NG * FEAT], BF16, name="xg")
+            st["xg", k] = xg
+            for a, z in cuts:
+                nc.sync.dma_start(
+                    out=xg[:, a * FEAT : z * FEAT].rearrange("p (t f) -> p t f", f=FEAT),
+                    in_=frame_rows(x, k)[:, a:z, :],
+                )
+
+        def load_p(k):
+            if k >= K:
+                return
+            xpi = xppool.tile([P, NP * FEAT], BF16, name="xpi")
+            st["xpi", k] = xpi
             nc.sync.dma_start(
-                out=x_sb[:],
-                in_=x[gi * ROWS : (gi + 1) * ROWS, :].rearrange("(p t) k -> p (t k)", t=T),
+                out=xpi[:].rearrange("p (t f) -> p t f", f=FEAT), in_=frame_rows(x, k)[:, NG:NU, :]
             )
-            return x_sb
 
-        x_tiles = [None] * GROUPS
-        x_tiles[0] = load_x(0)
+        def vertical(k, eng, cuts):
+            if k >= K:
+                return
+            u = upool.tile([P, NG * FEAT], F32, name="u")
+            st["u", k] = u
+            uv = u[:].rearrange(
+                "p (e t q v h j) -> p e v t q h j", e=2, t=4, q=4 * NG, v=2, h=2, j=8
+            )
+            for a, z in cuts:
+                xv = st["xg", k][:, a * FEAT : z * FEAT].rearrange(
+                    "p (q h t s j e) -> p s e t q h j", q=4 * (z - a), h=2, t=4, s=2, j=8, e=2
+                )
+                for e in (1, 0):
+                    for v in range(2):
+                        eng.tensor_tensor(
+                            out=uv[:, e, v, :, 4 * a : 4 * z],
+                            in0=xv[:, 0, e],
+                            in1=xv[:, 1, e],
+                            op=(ALU.add if v == 0 else ALU.subtract),
+                        )
 
-        w_sb = const.tile([P, 4, FEAT], BF16)
-        nc.sync.dma_start(out=w_sb[:], in_=W.rearrange("(a p) k -> p a k", p=P))
-        x_tiles[1] = load_x(1)
+        def pre_permute(k):
+            if k >= K:
+                return
+            xp = two.tile([P, NP * FEAT // 2], F32, name="xp")
+            st["xp", k] = xp
+            nc.scalar.copy(
+                out=xp[:].rearrange("p (t m c) -> p t m c", t=4, m=8 * NP, c=16),
+                in_=st["xpi", k][:]
+                .bitcast(F32)
+                .rearrange("p (m t c) -> p t m c", m=8 * NP, t=4, c=16),
+            )
+
+        def bank_of_eight(src, tiles, a, pool, tag):
+            bank = pool.tile([P, 8 * P], BF16, tag=tag, name="bank8")
+            for g in range(2):
+                for t in range(4):
+                    c0 = t * (tiles * 256) + a * 256 + g * P
+                    nc.tensor.transpose(
+                        bank[:, (g * 4 + t) * P : (g * 4 + t + 1) * P], src[:, c0 : c0 + P], ident[:]
+                    )
+            return bank
+
+        def t_p(k, p):
+            st["xtp", k, p] = bank_of_eight(st["xp", k][:].bitcast(BF16), NP, p, ps1, "xtp")
+
+        def x_copy(k, p):
+            x_t = two.tile([P, 8 * P], BF16, name="x_t")
+            st["x_t", k, p] = x_t
+            nc.scalar.copy(out=x_t[:], in_=st["xtp", k, p][:])
+
+        def haar_mm(k, p):
+            for g in range(2):
+                hp = ps2.tile([P, 512], F32, tag="hp", name="hp")
+                st["hp", k, p, g] = hp
+                nc.tensor.matmul(
+                    out=hp[:],
+                    lhsT=haar[:],
+                    rhs=st["x_t", k, p][:, g * 512 : (g + 1) * 512],
+                    start=True,
+                    stop=True,
+                )
+
+        def g_copy(k, p):
+            if p == 0:
+                st["gP", k] = one.tile([P, 2, NP * 512], BF16, align_bytes=64, name="gP")
+            for g in range(2):
+                nc.scalar.copy(
+                    out=st["gP", k][:, g, p * 512 : (p + 1) * 512].rearrange(
+                        "p (n t) -> p n t", t=4
+                    ),
+                    in_=st["hp", k, p, g][:].rearrange("p (t n) -> p n t", t=4),
+                )
+
+        def t_g(k, u):
+            for e in (1, 0):
+                if e == 1:
+                    bank = ps1.tile([P, 512], F32, tag="e1", name="e1")
+                else:
+                    bank = ps2.tile([P, 512], F32, tag="e0", name="e0")
+                st["e", k, u, e] = bank
+                for t in range(4):
+                    c0 = e * (NG * 512) + t * (NG * P) + u * P
+                    nc.tensor.transpose(
+                        bank[:, t * P : (t + 1) * P], st["u", k][:, c0 : c0 + P], ident_f[:]
+                    )
+
+        def e_copy(k, u):
+            e1h = two.tile([P, P, 4], F32, name="e1h")
+            st["e1h", k, u] = e1h
+            nc.scalar.activation(
+                out=e1h[:],
+                in_=st["e", k, u, 1][:].rearrange("p (t n) -> p n t", t=4),
+                func=ACT.Copy,
+                scale=0.5,
+            )
+
+        def horizontal(k, u):
+            if u == 0:
+                st["gG", k] = one.tile([P, 2, NG * 512], BF16, align_bytes=64, name="gG")
+            for h in range(2):
+                nc.vector.scalar_tensor_tensor(
+                    out=st["gG", k][:, h, u * 512 : (u + 1) * 512].rearrange(
+                        "p (n t) -> p n t", t=4
+                    ),
+                    in0=st["e", k, u, 0][:].rearrange("p (t n) -> p n t", t=4),
+                    scalar=0.5,
+                    in1=st["e1h", k, u][:],
+                    op0=ALU.mult,
+                    op1=(ALU.add if h == 0 else ALU.subtract),
+                )
+
+        def quantise(grouped, codes, scales, pieces):
+            for g in range(2):
+                for a, z in pieces:
+                    nc.vector.quantize_mx(
+                        out=codes[:, g, a:z].bitcast(FP8X4),
+                        scales=scales[:, g, a:z],
+                        in_=grouped[:, g, 4 * a : 4 * z],
+                    )
+
+        def q_kind(k, kind):
+            n = NG if kind == "G" else NP
+            codes = two.tile([P, 2, n * P], U32, align_bytes=64, name="c" + kind)
+            scales = two.tile([P, 2, n * P], U8, align_bytes=64, name="s" + kind)
+            st["c", kind, k] = (codes, scales)
+            pieces = [(0, 512), (512, 640)] if kind == "G" else [(0, 256), (256, 384)]
+            quantise(st["g" + kind, k], codes, scales, pieces)
+
+        def mx(k, kind, u):
+            codes, scales = st["c", kind, k]
+            w_codes, w_scales = st["w", kind]
+            acc = ps2.tile([P, OUT], F32, tag="acc", name="acc")
+            st["acc", k, kind, u] = acc
+            for g in range(2):
+                nc.tensor.matmul_mx(
+                    out=acc[:],
+                    lhsT=codes[:, g, u * P : (u + 1) * P].bitcast(FP8X4),
+                    lhsT_scale=scales[:, g, u * P : (u + 1) * P],
+                    rhs=w_codes[:, g, :].bitcast(FP8X4),
+                    rhs_scale=w_scales[:, g, :],
+                    start=(g == 0),
+                    stop=(g == 1),
+                )
+
+        def add_bias(k, kind, u):
+            if u == 0:
+                n = NG if kind == "G" else NP
+                st["o", kind, k] = two.tile(
+                    [P, n, OUT], F32, tag="o" + kind, align_bytes=64, name="o" + kind
+                )
+            nc.vector.tensor_tensor(
+                out=st["o", kind, k][:, u, :], in0=st["acc", k, kind, u][:], in1=bias[:], op=ALU.add
+            )
+
+        def store(k, kind):
+            a, z = (0, NG) if kind == "G" else (NG, NU)
+            nc.scalar.dma_start(out=frame_rows(out, k)[:, a:z, :], in_=st["o", kind, k][:])
+
+        load_g(0, [(0, 2), (2, NG)])
+        w_sb = const.tile([P, 4 * FEAT], BF16)
+        nc.sync.dma_start(
+            out=w_sb[:].rearrange("p (a f) -> p a f", f=FEAT),
+            in_=W.rearrange("(a p) f -> p a f", p=P),
+        )
+        load_p(0)
+        load_g(1, [(0, NG)])
         bias = const.tile([P, OUT], BF16)
         nc.sync.dma_start(out=bias[:], in_=b.partition_broadcast(P))
+        load_p(1)
+        for k in range(2, AHEAD):
+            load_g(k, [(0, NG)])
+            load_p(k)
 
         ident = const.tile([P, P], BF16)
         make_identity(nc, ident[:])
         ident_f = const.tile([P, P], F32)
         make_identity(nc, ident_f[:])
 
-        def transposes(src, tau):
-            xt = ps_w.tile([P, 2 * 4 * P], BF16, tag="w")
-            for g in range(2):
-                for t in range(4):
-                    c0 = t * (T * 256) + tau * 256 + g * P
-                    nc.tensor.transpose(
-                        xt[:, (g * 4 + t) * P : (g * 4 + t + 1) * P], src[:, c0 : c0 + P], ident[:]
-                    )
-            return xt
-
-        def quantise(grouped, codes, scales):
-            for g in range(2):
-                nc.vector.quantize_mx(
-                    out=codes[:, g, :].bitcast(FP8X4), scales=scales[:, g, :], in_=grouped[:, g, :]
-                )
-
-        def w_set(w_pm, name):
-            w_grouped = const.tile([P, 2, 4 * OUT], BF16, align_bytes=64, name="wg" + name)
-            w_codes = const.tile([P, 2, OUT], U32, align_bytes=64, name="wc" + name)
-            w_scales = const.tile([P, 2, OUT], U8, align_bytes=64, name="ws" + name)
-            for a in range(4):
-                xt = transposes(w_pm, a)
-                nc.vector.tensor_copy(
-                    out=w_grouped[:, :, a * 512 : (a + 1) * 512].rearrange(
-                        "p g (n t) -> p g n t", t=4
-                    ),
-                    in_=xt[:].rearrange("p (g t n) -> p g n t", g=2, t=4),
-                )
-            quantise(w_grouped, w_codes, w_scales)
-            return w_codes, w_scales
-
-        w_pm5 = const.tile([P, 4 * FEAT], BF16)
-        w5o = w_pm5[:].rearrange(
-            "p (t a h c r j) -> p t h a c r j", t=4, a=4, h=2, c=4, r=4, j=8
-        )
-        w5i = w_sb[:].rearrange("p a (c h r t j) -> p t h a c r j", c=4, h=2, r=4, t=4, j=8)
-        for t in range(4):
-            for h in range(2):
-                nc.scalar.copy(out=w5o[:, t, h], in_=w5i[:, t, h])
-        wc5, ws5 = w_set(w_pm5, "5")
-
-        w_pm4 = const.tile([P, 4 * FEAT], BF16)
-        w4o = w_pm4[:].rearrange("p (t a m j) -> p t a m j", t=4, a=4, m=32, j=8)
-        w4i = w_sb[:].rearrange("p a (m t j) -> p t a m j", m=32, t=4, j=8)
-        for t in range(4):
-            nc.scalar.copy(out=w4o[:, t], in_=w4i[:, t])
-        wc4, ws4 = w_set(w_pm4, "4")
+        vertical(0, nc.vector, [(0, 2), (2, NG)])
+        vertical(1, nc.gpsimd, [(0, NG)])
 
         h_a = const.tile([P, P], F32)
         iv = ident[:].rearrange("p (q h s c) -> p s q h c", q=2, h=2, s=2, c=16)
@@ -121,117 +259,118 @@ def tile_waveletlinearlayer_t_kernel(tc, x, W, b, out):
         haar = const.tile([P, P], BF16)
         nc.vector.tensor_scalar_mul(out=haar[:], in0=h_b[:], scalar1=0.5)
 
-        def front(gi):
-            x_sb = x_tiles[gi]
-            if KINDS[gi] == "G":
-                u = upool.tile([P, T * FEAT], F32)
-                xg = x_sb[:].rearrange(
-                    "p (q h t s j e) -> p s e t q h j", q=4 * T, h=2, t=4, s=2, j=8, e=2
-                )
-                uv = u[:].rearrange(
-                    "p (e t q v h j) -> p e v t q h j", e=2, t=4, q=4 * T, v=2, h=2, j=8
-                )
-                k = 0
-                for e in range(2):
-                    for v in range(2):
-                        eng = nc.vector if k < ON_VECTOR[gi] else nc.gpsimd
-                        eng.tensor_tensor(
-                            out=uv[:, e, v],
-                            in0=xg[:, 0, e],
-                            in1=xg[:, 1, e],
-                            op=(ALU.add if v == 0 else ALU.subtract),
-                        )
-                        k += 1
-                return u
-            xp = tpool.tile([P, T * FEAT // 2], F32)
-            nc.scalar.copy(
-                out=xp[:].rearrange("p (t m c) -> p t m c", t=4, m=8 * T, c=16),
-                in_=x_sb[:].bitcast(F32).rearrange("p (m t c) -> p t m c", m=8 * T, t=4, c=16),
-            )
-            return xp
+        w_words = w_sb[:].bitcast(F32)
+        w_pm = {}
+        w_pm["G"] = const.tile([P, 2 * FEAT], F32, name="w_pm_g")
+        w5o = w_pm["G"][:].rearrange(
+            "p (t a h c r j) -> p t h a c r j", t=4, a=4, h=2, c=4, r=4, j=4
+        )
+        w5i = w_words.rearrange("p (a c h r t j) -> p t h a c r j", a=4, c=4, h=2, r=4, t=4, j=4)
+        for t in range(4):
+            for h in range(2):
+                nc.scalar.copy(out=w5o[:, t, h], in_=w5i[:, t, h])
+        pre_permute(0)
+        w_pm["P"] = const.tile([P, 2 * FEAT], F32, name="w_pm_p")
+        w4o = w_pm["P"][:].rearrange("p (t a m j) -> p t a m j", t=4, a=4, m=32, j=4)
+        w4i = w_words.rearrange("p (a m t j) -> p t a m j", a=4, m=32, t=4, j=4)
+        for t in range(4):
+            nc.scalar.copy(out=w4o[:, t], in_=w4i[:, t])
 
-        def middle(gi, fr, grouped):
-            if KINDS[gi] == "G":
-                for tau in range(T):
-                    banks = []
-                    for e in range(2):
-                        bank = ps_w.tile([P, 512], F32, tag="w", name="bank")
-                        for t in range(4):
-                            c0 = e * (T * 512) + t * (T * P) + tau * P
-                            nc.tensor.transpose(
-                                bank[:, t * P : (t + 1) * P], fr[:, c0 : c0 + P], ident_f[:]
-                            )
-                        banks.append(bank)
-                    e1h = epool.tile([P, P, 4], F32)
-                    nc.scalar.activation(
-                        out=e1h[:],
-                        in_=banks[1][:].rearrange("p (t n) -> p n t", t=4),
-                        func=ACT.Copy,
-                        scale=0.5,
-                    )
-                    for h in range(2):
-                        nc.vector.scalar_tensor_tensor(
-                            out=grouped[:, h, tau * 512 : (tau + 1) * 512].rearrange(
-                                "p (n t) -> p n t", t=4
-                            ),
-                            in0=banks[0][:].rearrange("p (t n) -> p n t", t=4),
-                            scalar=0.5,
-                            in1=e1h[:],
-                            op0=ALU.mult,
-                            op1=(ALU.add if h == 0 else ALU.subtract),
-                        )
+        w_grouped = {}
+        w_bank_tags = [(ps1, "xtp"), (ps2, "hp"), (ps2, "hp")]
+        w_count = [0]
+
+        def w_tile(kind, a):
+            if a == 0:
+                w_grouped[kind] = two.tile(
+                    [P, 2, 4 * OUT], BF16, tag="oG", align_bytes=64, name="w_grouped"
+                )
+            pool, tag = w_bank_tags[w_count[0] % 3]
+            w_count[0] += 1
+            bank = bank_of_eight(w_pm[kind][:].bitcast(BF16), 4, a, pool, tag)
+            dst = w_grouped[kind][:, :, a * 512 : (a + 1) * 512].rearrange(
+                "p g (n t) -> p g n t", t=4
+            )
+            src = bank[:].rearrange("p (g t n) -> p g n t", g=2, t=4)
+            if kind == "G":
+                nc.vector.tensor_copy(out=dst, in_=src)
             else:
-                xpb = fr[:].bitcast(BF16)
-                for tau in range(T):
-                    xt = transposes(xpb, tau)
-                    x_t = xtpool.tile([P, 2 * 4 * P], BF16)
-                    nc.scalar.copy(out=x_t[:], in_=xt[:])
-                    for g in range(2):
-                        hp = ps_w.tile([P, 512], F32, tag="w")
-                        nc.tensor.matmul(
-                            out=hp[:],
-                            lhsT=haar[:],
-                            rhs=x_t[:, g * 512 : (g + 1) * 512],
-                            start=True,
-                            stop=True,
-                        )
-                        nc.scalar.copy(
-                            out=grouped[:, g, tau * 512 : (tau + 1) * 512].rearrange(
-                                "p (n t) -> p n t", t=4
-                            ),
-                            in_=hp[:].rearrange("p (t n) -> p n t", t=4),
-                        )
+                nc.scalar.copy(out=dst, in_=src)
 
-        fronts = [None] * GROUPS
-        fronts[0] = front(0)
-        for gi in range(GROUPS):
-            for nxt in range(gi + 1, min(gi + 4, GROUPS)):
-                if x_tiles[nxt] is None:
-                    x_tiles[nxt] = load_x(nxt)
-            if gi + 1 < GROUPS:
-                fronts[gi + 1] = front(gi + 1)
-            grouped = gpool.tile([P, 2, T * 512], BF16, align_bytes=64)
-            codes = cpool.tile([P, 2, T * P], U32, align_bytes=64)
-            scales = cpool.tile([P, 2, T * P], U8, align_bytes=64)
-            middle(gi, fronts[gi], grouped)
-            quantise(grouped, codes, scales)
-            w_codes, w_scales = (wc5, ws5) if KINDS[gi] == "G" else (wc4, ws4)
+        def w_quantise(kind):
+            w_codes = const.tile([P, 2, OUT], U32, align_bytes=64, name="wc" + kind)
+            w_scales = const.tile([P, 2, OUT], U8, align_bytes=64, name="ws" + kind)
+            st["w", kind] = (w_codes, w_scales)
+            quantise(w_grouped[kind], w_codes, w_scales, [(0, 512)])
 
-            o_sb = opool.tile([P, T, OUT], F32)
-            for tau in range(T):
-                acc = ps_a.tile([P, OUT], F32)
-                for g in range(2):
-                    nc.tensor.matmul_mx(
-                        out=acc[:],
-                        lhsT=codes[:, g, tau * P : (tau + 1) * P].bitcast(FP8X4),
-                        lhsT_scale=scales[:, g, tau * P : (tau + 1) * P],
-                        rhs=w_codes[:, g, :].bitcast(FP8X4),
-                        rhs_scale=w_scales[:, g, :],
-                        start=(g == 0),
-                        stop=(g == 1),
-                    )
-                nc.vector.tensor_tensor(out=o_sb[:, tau, :], in0=acc[:], in1=bias[:], op=ALU.add)
-            nc.sync.dma_start(
-                out=out[gi * ROWS : (gi + 1) * ROWS, :].rearrange("(p t) o -> p t o", t=T),
-                in_=o_sb[:],
-            )
+        units = [("P", p) for p in range(NP)] + [("G", u) for u in range(NG)]
+
+        for k in range(K + 2):
+            cur = k < K
+            prv = 1 <= k <= K
+            load_g(k + AHEAD, [(0, NG)])
+            load_p(k + AHEAD)
+            if k >= 1:
+                vertical(k + 1, nc.gpsimd, [(0, NG)])
+
+            def finish(a, z):
+                if prv:
+                    for kind, u in units[a:z]:
+                        mx(k - 1, kind, u)
+                    for kind, u in units[a:z]:
+                        add_bias(k - 1, kind, u)
+                if k == 0:
+                    kind = "G" if a < 4 else "P"
+                    w_tile(kind, a % 4)
+                    w_tile(kind, a % 4 + 1)
+                    if a % 4 == 2:
+                        w_quantise(kind)
+
+            def start_g(u):
+                if cur:
+                    t_g(k, u)
+                    e_copy(k, u)
+
+            def start_p(p):
+                if cur:
+                    t_p(k, p)
+                    x_copy(k, p)
+
+            def mid_p(p):
+                if cur:
+                    haar_mm(k, p)
+                    g_copy(k, p)
+
+            def end_g(u):
+                if cur:
+                    horizontal(k, u)
+
+            start_g(0)
+            start_p(0)
+            if k >= 2:
+                store(k - 2, "G")
+            end_g(0)
+            finish(0, 2)
+            start_g(1)
+            mid_p(0)
+            start_p(1)
+            end_g(1)
+            finish(2, 4)
+            start_g(2)
+            mid_p(1)
+            start_p(2)
+            end_g(2)
+            finish(4, 6)
+            if prv:
+                store(k - 1, "P")
+            start_g(3)
+            mid_p(2)
+            end_g(3)
+            if cur:
+                q_kind(k, "P")
+            finish(6, 8)
+            start_g(4)
+            pre_permute(k + 1)
+            end_g(4)
+            if cur:
+                q_kind(k, "G")

@@ -23,6 +23,7 @@ FRAME = NU * P
 K = 8192 // FRAME
 AHEAD = 3
 PINNED = True
+POOL_OUT = [("G", 4)]
 
 
 def tile_waveletlinearlayer_t_kernel(tc, x, W, b, out):
@@ -67,8 +68,9 @@ def tile_waveletlinearlayer_t_kernel(tc, x, W, b, out):
         def vertical(k, eng, cuts):
             if k >= K:
                 return
-            u = upool.tile([P, NG * FEAT], F32, name="u")
-            st["u", k] = u
+            if ("u", k) not in st:
+                st["u", k] = upool.tile([P, NG * FEAT], F32, name="u")
+            u = st["u", k]
             uv = u[:].rearrange(
                 "p (e t q v h j) -> p e v t q h j", e=2, t=4, q=4 * NG, v=2, h=2, j=8
             )
@@ -185,12 +187,13 @@ def tile_waveletlinearlayer_t_kernel(tc, x, W, b, out):
                         in_=grouped[:, g, 4 * a : 4 * z],
                     )
 
-        def q_kind(k, kind):
+        def q_kind(k, kind, pieces):
             n = NG if kind == "G" else NP
-            codes = two.tile([P, 2, n * P], U32, align_bytes=64, name="c" + kind)
-            scales = two.tile([P, 2, n * P], U8, align_bytes=64, name="s" + kind)
-            st["c", kind, k] = (codes, scales)
-            pieces = [(0, 512), (512, 640)] if kind == "G" else [(0, 256), (256, 384)]
+            if ("c", kind, k) not in st:
+                codes = two.tile([P, 2, n * P], U32, align_bytes=64, name="c" + kind)
+                scales = two.tile([P, 2, n * P], U8, align_bytes=64, name="s" + kind)
+                st["c", kind, k] = (codes, scales)
+            codes, scales = st["c", kind, k]
             quantise(st["g" + kind, k], codes, scales, pieces)
 
         def mx(k, kind, u):
@@ -215,13 +218,18 @@ def tile_waveletlinearlayer_t_kernel(tc, x, W, b, out):
                 st["o", kind, k] = two.tile(
                     [P, n, OUT], F32, tag="o" + kind, align_bytes=64, name="o" + kind
                 )
-            nc.vector.tensor_tensor(
-                out=st["o", kind, k][:, u, :], in0=st["acc", k, kind, u][:], in1=bias[:], op=ALU.add
-            )
+            dst = st["o", kind, k][:, u, :]
+            if (kind, u) in POOL_OUT:
+                nc.scalar.copy(out=dst, in_=st["acc", k, kind, u][:])
+                nc.gpsimd.tensor_tensor(out=dst, in0=dst, in1=bias[:], op=ALU.add)
+            else:
+                nc.vector.tensor_tensor(out=dst, in0=st["acc", k, kind, u][:], in1=bias[:], op=ALU.add)
 
-        def store(k, kind):
-            a, z = (0, NG) if kind == "G" else (NG, NU)
-            nc.scalar.dma_start(out=frame_rows(out, k)[:, a:z, :], in_=st["o", kind, k][:])
+        def store(k, kind, a, z):
+            base = 0 if kind == "G" else NG
+            nc.scalar.dma_start(
+                out=frame_rows(out, k)[:, base + a : base + z, :], in_=st["o", kind, k][:, a:z, :]
+            )
 
         load_g(0, [(0, 2), (2, NG)])
         w_sb = const.tile([P, 4 * FEAT], BF16)
@@ -243,7 +251,8 @@ def tile_waveletlinearlayer_t_kernel(tc, x, W, b, out):
         ident_f = const.tile([P, P], F32)
         make_identity(nc, ident_f[:])
 
-        vertical(0, nc.vector, [(0, 2), (2, NG)])
+        vertical(0, nc.vector, [(0, 2)])
+        vertical(0, nc.gpsimd, [(2, NG)])
         vertical(1, nc.gpsimd, [(0, NG)])
 
         h_a = const.tile([P, P], F32)
@@ -305,7 +314,7 @@ def tile_waveletlinearlayer_t_kernel(tc, x, W, b, out):
 
         units = [("P", p) for p in range(NP)] + [("G", u) for u in range(NG)]
 
-        for k in range(K + 2):
+        for k in range(K + 1):
             cur = k < K
             prv = 1 <= k <= K
             load_g(k + AHEAD, [(0, NG)])
@@ -347,8 +356,8 @@ def tile_waveletlinearlayer_t_kernel(tc, x, W, b, out):
 
             start_g(0)
             start_p(0)
-            if k >= 2:
-                store(k - 2, "G")
+            if 2 <= k <= K:
+                store(k - 2, "G", 0, NG)
             end_g(0)
             finish(0, 2)
             start_g(1)
@@ -362,15 +371,20 @@ def tile_waveletlinearlayer_t_kernel(tc, x, W, b, out):
             end_g(2)
             finish(4, 6)
             if prv:
-                store(k - 1, "P")
+                store(k - 1, "P", 0, NP)
+            if k == K:
+                store(k - 1, "G", 0, 3)
             start_g(3)
             mid_p(2)
             end_g(3)
             if cur:
-                q_kind(k, "P")
+                q_kind(k, "P", [(0, 256), (256, 384)])
+                q_kind(k, "G", [(0, 512)])
             finish(6, 8)
+            if k == K:
+                store(k - 1, "G", 3, NG)
             start_g(4)
             pre_permute(k + 1)
             end_g(4)
             if cur:
-                q_kind(k, "G")
+                q_kind(k, "G", [(512, 640)])

@@ -16,375 +16,362 @@ FLOPS = 2 * 8192 * 1024 * 512
 P = 128
 FEAT = 1024
 OUT = 512
-NG = 5
-NP = 3
-NU = NG + NP
-FRAME = NU * P
-K = 8192 // FRAME
+SLOTS = 4
+PASSES = 2
+BANK = 512
+N_ADD = 5
+N_MM = 3
+N_TILES = N_ADD + N_MM
+FRAME = N_TILES * P
+FRAMES = 8192 // FRAME
 AHEAD = 3
-PINNED = True
-POOL_OUT = [("G", 4)]
 
 
 def tile_waveletlinearlayer_t_kernel(tc, x, W, b, out):
     nc = tc.nc
     with ExitStack() as ctx:
         const = ctx.enter_context(tc.tile_pool(name="const", bufs=1))
-        xgpool = ctx.enter_context(tc.tile_pool(name="xgpool", bufs=3))
-        xppool = ctx.enter_context(tc.tile_pool(name="xppool", bufs=3))
-        upool = ctx.enter_context(tc.tile_pool(name="upool", bufs=2))
+        x_pool = ctx.enter_context(tc.tile_pool(name="x_pool", bufs=AHEAD))
         two = ctx.enter_context(tc.tile_pool(name="two", bufs=2))
-        one = ctx.enter_context(tc.tile_pool(name="one", bufs=1))
-        ps1 = ctx.enter_context(tc.psum_pool(name="ps1", bufs=1))
-        ps2 = ctx.enter_context(tc.psum_pool(name="ps2", bufs=2))
-        if PINNED:
-            ctx.enter_context(tc.manual_schedule())
+        psum_one = ctx.enter_context(tc.psum_pool(name="psum_one", bufs=1))
+        psum_two = ctx.enter_context(tc.psum_pool(name="psum_two", bufs=2))
+        ctx.enter_context(tc.manual_schedule())
 
-        st = {}
+        live = {}
 
         def frame_rows(ap, k):
-            return ap[k * FRAME : (k + 1) * FRAME, :].rearrange("(p t) f -> p t f", t=NU)
+            return ap[k * FRAME : (k + 1) * FRAME, :].rearrange("(p r) f -> p r f", r=N_TILES)
 
-        def load_g(k, cuts):
-            if k >= K:
+        def load(k, cuts):
+            if k >= FRAMES:
                 return
-            xg = xgpool.tile([P, NG * FEAT], BF16, name="xg")
-            st["xg", k] = xg
+            x_add = x_pool.tile([P, N_ADD * FEAT], BF16, name="x_add")
+            x_mm = x_pool.tile([P, N_MM * FEAT], BF16, name="x_mm")
+            live["x_add", k] = x_add
+            live["x_mm", k] = x_mm
             for a, z in cuts:
                 nc.sync.dma_start(
-                    out=xg[:, a * FEAT : z * FEAT].rearrange("p (t f) -> p t f", f=FEAT),
+                    out=x_add[:, a * FEAT : z * FEAT].rearrange("p (r f) -> p r f", f=FEAT),
                     in_=frame_rows(x, k)[:, a:z, :],
                 )
 
-        def load_p(k):
-            if k >= K:
+        def load_mm(k):
+            if k >= FRAMES:
                 return
-            xpi = xppool.tile([P, NP * FEAT], BF16, name="xpi")
-            st["xpi", k] = xpi
             nc.sync.dma_start(
-                out=xpi[:].rearrange("p (t f) -> p t f", f=FEAT), in_=frame_rows(x, k)[:, NG:NU, :]
+                out=live["x_mm", k][:].rearrange("p (r f) -> p r f", f=FEAT),
+                in_=frame_rows(x, k)[:, N_ADD:N_TILES, :],
             )
 
-        def vertical(k, eng, cuts):
-            if k >= K:
+        def vertical(k, engine, cuts):
+            if k >= FRAMES:
                 return
-            if ("u", k) not in st:
-                st["u", k] = upool.tile([P, NG * FEAT], F32, name="u")
-            u = st["u", k]
-            uv = u[:].rearrange(
-                "p (e t q v h j) -> p e v t q h j", e=2, t=4, q=4 * NG, v=2, h=2, j=8
+            u = two.tile([P, N_ADD * FEAT], F32, name="u")
+            live["u", k] = u
+            u_view = u[:].rearrange(
+                "p (e t q v h j) -> p e v t q h j", e=2, t=4, q=4 * N_ADD, v=2, h=2, j=8
             )
             for a, z in cuts:
-                xv = st["xg", k][:, a * FEAT : z * FEAT].rearrange(
+                x_view = live["x_add", k][:, a * FEAT : z * FEAT].rearrange(
                     "p (q h t s j e) -> p s e t q h j", q=4 * (z - a), h=2, t=4, s=2, j=8, e=2
                 )
                 for e in (1, 0):
                     for v in range(2):
-                        eng.tensor_tensor(
-                            out=uv[:, e, v, :, 4 * a : 4 * z],
-                            in0=xv[:, 0, e],
-                            in1=xv[:, 1, e],
+                        engine.tensor_tensor(
+                            out=u_view[:, e, v, :, 4 * a : 4 * z],
+                            in0=x_view[:, 0, e],
+                            in1=x_view[:, 1, e],
                             op=(ALU.add if v == 0 else ALU.subtract),
                         )
 
-        def pre_permute(k):
-            if k >= K:
-                return
-            xp = two.tile([P, NP * FEAT // 2], F32, name="xp")
-            st["xp", k] = xp
-            nc.scalar.copy(
-                out=xp[:].rearrange("p (t m c) -> p t m c", t=4, m=8 * NP, c=16),
-                in_=st["xpi", k][:]
-                .bitcast(F32)
-                .rearrange("p (m t c) -> p t m c", m=8 * NP, t=4, c=16),
-            )
-
-        def bank_of_eight(src, tiles, a, pool, tag):
-            bank = pool.tile([P, 8 * P], BF16, tag=tag, name="bank8")
-            for g in range(2):
-                for t in range(4):
-                    c0 = t * (tiles * 256) + a * 256 + g * P
-                    nc.tensor.transpose(
-                        bank[:, (g * 4 + t) * P : (g * 4 + t + 1) * P], src[:, c0 : c0 + P], ident[:]
-                    )
-            return bank
-
-        def t_p(k, p):
-            st["xtp", k, p] = bank_of_eight(st["xp", k][:].bitcast(BF16), NP, p, ps1, "xtp")
-
-        def x_copy(k, p):
-            x_t = two.tile([P, 8 * P], BF16, name="x_t")
-            st["x_t", k, p] = x_t
-            nc.scalar.copy(out=x_t[:], in_=st["xtp", k, p][:])
-
-        def haar_mm(k, p):
-            for g in range(2):
-                hp = ps2.tile([P, 512], F32, tag="hp", name="hp")
-                st["hp", k, p, g] = hp
-                nc.tensor.matmul(
-                    out=hp[:],
-                    lhsT=haar[:],
-                    rhs=st["x_t", k, p][:, g * 512 : (g + 1) * 512],
-                    start=True,
-                    stop=True,
-                )
-
-        def g_copy(k, p):
-            if p == 0:
-                st["gP", k] = one.tile([P, 2, NP * 512], BF16, align_bytes=64, name="gP")
-            for g in range(2):
-                nc.scalar.copy(
-                    out=st["gP", k][:, g, p * 512 : (p + 1) * 512].rearrange(
-                        "p (n t) -> p n t", t=4
-                    ),
-                    in_=st["hp", k, p, g][:].rearrange("p (t n) -> p n t", t=4),
-                )
-
-        def t_g(k, u):
+        def turn_add(k, r):
             for e in (1, 0):
                 if e == 1:
-                    bank = ps1.tile([P, 512], F32, tag="e1", name="e1")
+                    bank = psum_one.tile([P, BANK], F32, name="odd")
                 else:
-                    bank = ps2.tile([P, 512], F32, tag="e0", name="e0")
-                st["e", k, u, e] = bank
-                for t in range(4):
-                    c0 = e * (NG * 512) + t * (NG * P) + u * P
+                    bank = psum_two.tile([P, BANK], F32, name="even")
+                live["bank", k, r, e] = bank
+                for t in range(SLOTS):
+                    c0 = e * (N_ADD * BANK) + t * (N_ADD * P) + r * P
                     nc.tensor.transpose(
-                        bank[:, t * P : (t + 1) * P], st["u", k][:, c0 : c0 + P], ident_f[:]
+                        bank[:, t * P : (t + 1) * P], live["u", k][:, c0 : c0 + P], ident_f32[:]
                     )
-
-        def e_copy(k, u):
-            e1h = two.tile([P, P, 4], F32, name="e1h")
-            st["e1h", k, u] = e1h
+            odd_half = two.tile([P, P, SLOTS], F32, name="odd_half")
+            live["odd_half", k, r] = odd_half
             nc.scalar.activation(
-                out=e1h[:],
-                in_=st["e", k, u, 1][:].rearrange("p (t n) -> p n t", t=4),
+                out=odd_half[:],
+                in_=live["bank", k, r, 1][:].rearrange("p (t n) -> p n t", t=SLOTS),
                 func=ACT.Copy,
                 scale=0.5,
             )
 
-        def horizontal(k, u):
-            if u == 0:
-                st["gG", k] = one.tile([P, 2, NG * 512], BF16, align_bytes=64, name="gG")
-            for h in range(2):
+        def horizontal(k, r):
+            for h in range(PASSES):
                 nc.vector.scalar_tensor_tensor(
-                    out=st["gG", k][:, h, u * 512 : (u + 1) * 512].rearrange(
-                        "p (n t) -> p n t", t=4
+                    out=grouped["add"][:, h, r * BANK : (r + 1) * BANK].rearrange(
+                        "p (n t) -> p n t", t=SLOTS
                     ),
-                    in0=st["e", k, u, 0][:].rearrange("p (t n) -> p n t", t=4),
+                    in0=live["bank", k, r, 0][:].rearrange("p (t n) -> p n t", t=SLOTS),
                     scalar=0.5,
-                    in1=st["e1h", k, u][:],
+                    in1=live["odd_half", k, r][:],
                     op0=ALU.mult,
                     op1=(ALU.add if h == 0 else ALU.subtract),
                 )
 
-        def quantise(grouped, codes, scales, pieces):
-            for g in range(2):
-                for a, z in pieces:
-                    nc.vector.quantize_mx(
-                        out=codes[:, g, a:z].bitcast(FP8X4),
-                        scales=scales[:, g, a:z],
-                        in_=grouped[:, g, 4 * a : 4 * z],
-                    )
+        def gather_blocks(k):
+            if k >= FRAMES:
+                return
+            x_sorted = two.tile([P, N_MM * FEAT // 2], F32, name="x_sorted")
+            live["x_sorted", k] = x_sorted
+            nc.scalar.copy(
+                out=x_sorted[:].rearrange("p (t m c) -> p t m c", t=4, m=8 * N_MM, c=16),
+                in_=live["x_mm", k][:]
+                .bitcast(F32)
+                .rearrange("p (m t c) -> p t m c", m=8 * N_MM, t=4, c=16),
+            )
 
-        def q_kind(k, kind, pieces):
-            n = NG if kind == "G" else NP
-            if ("c", kind, k) not in st:
-                codes = two.tile([P, 2, n * P], U32, align_bytes=64, name="c" + kind)
-                scales = two.tile([P, 2, n * P], U8, align_bytes=64, name="s" + kind)
-                st["c", kind, k] = (codes, scales)
-            codes, scales = st["c", kind, k]
-            quantise(st["g" + kind, k], codes, scales, pieces)
+        def eight_transposes(src, row_tiles, r, pool, tag):
+            bank = pool.tile([P, PASSES * SLOTS * P], BF16, tag=tag, name="turned")
+            for g in range(PASSES):
+                for t in range(SLOTS):
+                    c0 = t * (row_tiles * PASSES * P) + r * PASSES * P + g * P
+                    c1 = (g * SLOTS + t) * P
+                    nc.tensor.transpose(bank[:, c1 : c1 + P], src[:, c0 : c0 + P], ident[:])
+            return bank
 
-        def mx(k, kind, u):
-            codes, scales = st["c", kind, k]
-            w_codes, w_scales = st["w", kind]
-            acc = ps2.tile([P, OUT], F32, tag="acc", name="acc")
-            st["acc", k, kind, u] = acc
-            for g in range(2):
+        def turn_mm(k, r):
+            bank = eight_transposes(live["x_sorted", k][:].bitcast(BF16), N_MM, r, psum_one, "turned")
+            x_turned = two.tile([P, PASSES * SLOTS * P], BF16, name="x_turned")
+            live["x_turned", k, r] = x_turned
+            nc.scalar.copy(out=x_turned[:], in_=bank[:])
+
+        def haar_mm(k, r):
+            for g in range(PASSES):
+                bank = psum_two.tile([P, BANK], F32, name="haar_out")
+                nc.tensor.matmul(
+                    out=bank[:],
+                    lhsT=haar[:],
+                    rhs=live["x_turned", k, r][:, g * BANK : (g + 1) * BANK],
+                    start=True,
+                    stop=True,
+                )
+                nc.scalar.copy(
+                    out=grouped["mm"][:, g, r * BANK : (r + 1) * BANK].rearrange(
+                        "p (n t) -> p n t", t=SLOTS
+                    ),
+                    in_=bank[:].rearrange("p (t n) -> p n t", t=SLOTS),
+                )
+
+        def quantise(values, codes, scales, a, z):
+            for g in range(PASSES):
+                nc.vector.quantize_mx(
+                    out=codes[:, g, a:z].bitcast(FP8X4),
+                    scales=scales[:, g, a:z],
+                    in_=values[:, g, SLOTS * a : SLOTS * z],
+                )
+
+        def quantise_t(k, way, a, z):
+            if a == 0:
+                n = N_ADD if way == "add" else N_MM
+                live["codes", way, k] = (
+                    two.tile([P, PASSES, n * P], U32, align_bytes=64, name="codes_" + way),
+                    two.tile([P, PASSES, n * P], U8, align_bytes=64, name="scales_" + way),
+                )
+            codes, scales = live["codes", way, k]
+            quantise(grouped[way], codes, scales, a, z)
+
+        def multiply(k, way, r):
+            codes, scales = live["codes", way, k]
+            w_codes, w_scales = w_mx[way]
+            acc = psum_two.tile([P, OUT], F32, name="acc")
+            live["acc", k, way, r] = acc
+            for g in range(PASSES):
                 nc.tensor.matmul_mx(
                     out=acc[:],
-                    lhsT=codes[:, g, u * P : (u + 1) * P].bitcast(FP8X4),
-                    lhsT_scale=scales[:, g, u * P : (u + 1) * P],
+                    lhsT=codes[:, g, r * P : (r + 1) * P].bitcast(FP8X4),
+                    lhsT_scale=scales[:, g, r * P : (r + 1) * P],
                     rhs=w_codes[:, g, :].bitcast(FP8X4),
                     rhs_scale=w_scales[:, g, :],
                     start=(g == 0),
-                    stop=(g == 1),
+                    stop=(g == PASSES - 1),
                 )
 
-        def add_bias(k, kind, u):
-            if u == 0:
-                n = NG if kind == "G" else NP
-                st["o", kind, k] = two.tile(
-                    [P, n, OUT], F32, tag="o" + kind, align_bytes=64, name="o" + kind
+        def add_bias(k, way, r):
+            if r == 0:
+                n = N_ADD if way == "add" else N_MM
+                live["result", way, k] = two.tile(
+                    [P, n, OUT], F32, tag="result_" + way, align_bytes=64, name="result"
                 )
-            dst = st["o", kind, k][:, u, :]
-            if (kind, u) in POOL_OUT:
-                nc.scalar.copy(out=dst, in_=st["acc", k, kind, u][:])
-                nc.gpsimd.tensor_tensor(out=dst, in0=dst, in1=bias[:], op=ALU.add)
-            else:
-                nc.vector.tensor_tensor(out=dst, in0=st["acc", k, kind, u][:], in1=bias[:], op=ALU.add)
+            nc.vector.tensor_tensor(
+                out=live["result", way, k][:, r, :],
+                in0=live["acc", k, way, r][:],
+                in1=bias[:],
+                op=ALU.add,
+            )
 
-        def store(k, kind, a, z):
-            base = 0 if kind == "G" else NG
+        def store(k, way, a, z):
+            first = 0 if way == "add" else N_ADD
             nc.scalar.dma_start(
-                out=frame_rows(out, k)[:, base + a : base + z, :], in_=st["o", kind, k][:, a:z, :]
+                out=frame_rows(out, k)[:, first + a : first + z, :],
+                in_=live["result", way, k][:, a:z, :],
             )
 
-        load_g(0, [(0, 2), (2, NG)])
-        w_sb = const.tile([P, 4 * FEAT], BF16)
-        nc.sync.dma_start(
-            out=w_sb[:].rearrange("p (a f) -> p a f", f=FEAT),
-            in_=W.rearrange("(a p) f -> p a f", p=P),
-        )
-        load_p(0)
-        load_g(1, [(0, NG)])
-        bias = const.tile([P, OUT], BF16)
-        nc.sync.dma_start(out=bias[:], in_=b.partition_broadcast(P))
-        load_p(1)
-        for k in range(2, AHEAD):
-            load_g(k, [(0, NG)])
-            load_p(k)
-
-        ident = const.tile([P, P], BF16)
-        make_identity(nc, ident[:])
-        ident_f = const.tile([P, P], F32)
-        make_identity(nc, ident_f[:])
-
-        vertical(0, nc.vector, [(0, 2)])
-        vertical(0, nc.gpsimd, [(2, NG)])
-        vertical(1, nc.gpsimd, [(0, NG)])
-
-        h_a = const.tile([P, P], F32)
-        iv = ident[:].rearrange("p (q h s c) -> p s q h c", q=2, h=2, s=2, c=16)
-        av = h_a[:].rearrange("p (q v h c) -> p v q h c", q=2, v=2, h=2, c=16)
-        nc.vector.tensor_tensor(out=av[:, 0], in0=iv[:, 0], in1=iv[:, 1], op=ALU.add)
-        nc.vector.tensor_tensor(out=av[:, 1], in0=iv[:, 0], in1=iv[:, 1], op=ALU.subtract)
-        h_b = const.tile([P, P], F32)
-        ae = h_a[:].rearrange("p (w r e) -> p e w r", r=32, e=2)
-        hv = h_b[:].rearrange("p (w h r) -> p h w r", h=2, r=32)
-        nc.vector.tensor_tensor(out=hv[:, 0], in0=ae[:, 0], in1=ae[:, 1], op=ALU.add)
-        nc.vector.tensor_tensor(out=hv[:, 1], in0=ae[:, 0], in1=ae[:, 1], op=ALU.subtract)
-        haar = const.tile([P, P], BF16)
-        nc.vector.tensor_scalar_mul(out=haar[:], in0=h_b[:], scalar1=0.5)
-
-        w_words = w_sb[:].bitcast(F32)
-        w_pm = {}
-        w_pm["G"] = const.tile([P, 2 * FEAT], F32, name="w_pm_g")
-        w5o = w_pm["G"][:].rearrange(
-            "p (t a h c r j) -> p t h a c r j", t=4, a=4, h=2, c=4, r=4, j=4
-        )
-        w5i = w_words.rearrange("p (a c h r t j) -> p t h a c r j", a=4, c=4, h=2, r=4, t=4, j=4)
-        for t in range(4):
-            for h in range(2):
-                nc.scalar.copy(out=w5o[:, t, h], in_=w5i[:, t, h])
-        pre_permute(0)
-        w_pm["P"] = const.tile([P, 2 * FEAT], F32, name="w_pm_p")
-        w4o = w_pm["P"][:].rearrange("p (t a m j) -> p t a m j", t=4, a=4, m=32, j=4)
-        w4i = w_words.rearrange("p (a m t j) -> p t a m j", a=4, m=32, t=4, j=4)
-        for t in range(4):
-            nc.scalar.copy(out=w4o[:, t], in_=w4i[:, t])
-
-        w_grouped = {}
-        w_bank_tags = [(ps1, "xtp"), (ps2, "hp"), (ps2, "hp")]
-        w_count = [0]
-
-        def w_tile(kind, a):
-            if a == 0:
-                w_grouped[kind] = two.tile(
-                    [P, 2, 4 * OUT], BF16, tag="oG", align_bytes=64, name="w_grouped"
+        def sort_w(way):
+            w_sorted[way] = const.tile([P, 2 * FEAT], F32, name="w_sorted_" + way)
+            words = w_rows[:].bitcast(F32)
+            if way == "add":
+                dst = w_sorted[way][:].rearrange(
+                    "p (t a h c r j) -> p t h a c r j", t=4, a=4, h=2, c=4, r=4, j=4
                 )
-            pool, tag = w_bank_tags[w_count[0] % 3]
-            w_count[0] += 1
-            bank = bank_of_eight(w_pm[kind][:].bitcast(BF16), 4, a, pool, tag)
-            dst = w_grouped[kind][:, :, a * 512 : (a + 1) * 512].rearrange(
-                "p g (n t) -> p g n t", t=4
+                src = words.rearrange(
+                    "p (a c h r t j) -> p t h a c r j", a=4, c=4, h=2, r=4, t=4, j=4
+                )
+                for t in range(SLOTS):
+                    for h in range(PASSES):
+                        nc.scalar.copy(out=dst[:, t, h], in_=src[:, t, h])
+            else:
+                dst = w_sorted[way][:].rearrange("p (t a m j) -> p t a m j", t=4, a=4, m=32, j=4)
+                src = words.rearrange("p (a m t j) -> p t a m j", a=4, m=32, t=4, j=4)
+                for t in range(SLOTS):
+                    nc.scalar.copy(out=dst[:, t], in_=src[:, t])
+
+        def turn_w(way, a):
+            if a == 0:
+                w_grouped[way] = two.tile(
+                    [P, PASSES, SLOTS * OUT], BF16, tag="result_add", align_bytes=64, name="w_grouped"
+                )
+            pool, tag = ((psum_one, "turned"), (psum_two, "haar_out"))[a % 2]
+            bank = eight_transposes(w_sorted[way][:].bitcast(BF16), 4, a, pool, tag)
+            dst = w_grouped[way][:, :, a * BANK : (a + 1) * BANK].rearrange(
+                "p g (n t) -> p g n t", t=SLOTS
             )
-            src = bank[:].rearrange("p (g t n) -> p g n t", g=2, t=4)
-            if kind == "G":
+            src = bank[:].rearrange("p (g t n) -> p g n t", g=PASSES, t=SLOTS)
+            if way == "add":
                 nc.vector.tensor_copy(out=dst, in_=src)
             else:
                 nc.scalar.copy(out=dst, in_=src)
 
-        def w_quantise(kind):
-            w_codes = const.tile([P, 2, OUT], U32, align_bytes=64, name="wc" + kind)
-            w_scales = const.tile([P, 2, OUT], U8, align_bytes=64, name="ws" + kind)
-            st["w", kind] = (w_codes, w_scales)
-            quantise(w_grouped[kind], w_codes, w_scales, [(0, 512)])
+        def quantise_w(way):
+            w_mx[way] = (
+                const.tile([P, PASSES, OUT], U32, align_bytes=64, name="w_codes_" + way),
+                const.tile([P, PASSES, OUT], U8, align_bytes=64, name="w_scales_" + way),
+            )
+            quantise(w_grouped[way], w_mx[way][0], w_mx[way][1], 0, OUT)
 
-        units = [("P", p) for p in range(NP)] + [("G", u) for u in range(NG)]
+        load(0, [(0, 2), (2, N_ADD)])
+        w_rows = const.tile([P, 4 * FEAT], BF16)
+        nc.sync.dma_start(
+            out=w_rows[:].rearrange("p (a f) -> p a f", f=FEAT),
+            in_=W.rearrange("(a p) f -> p a f", p=P),
+        )
+        load_mm(0)
+        load(1, [(0, N_ADD)])
+        bias = const.tile([P, OUT], BF16)
+        nc.sync.dma_start(out=bias[:], in_=b.partition_broadcast(P))
+        load_mm(1)
+        for k in range(2, AHEAD):
+            load(k, [(0, N_ADD)])
+            load_mm(k)
 
-        for k in range(K + 1):
-            cur = k < K
-            prv = 1 <= k <= K
-            load_g(k + AHEAD, [(0, NG)])
-            load_p(k + AHEAD)
-            if k >= 1:
-                vertical(k + 1, nc.gpsimd, [(0, NG)])
+        ident = const.tile([P, P], BF16)
+        make_identity(nc, ident[:])
+        ident_f32 = const.tile([P, P], F32)
+        make_identity(nc, ident_f32[:])
 
-            def finish(a, z):
-                if prv:
-                    for kind, u in units[a:z]:
-                        mx(k - 1, kind, u)
-                    for kind, u in units[a:z]:
-                        add_bias(k - 1, kind, u)
-                if k == 0:
-                    kind = "G" if a < 4 else "P"
-                    w_tile(kind, a % 4)
-                    w_tile(kind, a % 4 + 1)
+        vertical(0, nc.vector, [(0, 2), (2, N_ADD)])
+        vertical(1, nc.gpsimd, [(0, N_ADD)])
+
+        stage1 = const.tile([P, P], F32)
+        i_view = ident[:].rearrange("p (q h s c) -> p s q h c", q=2, h=2, s=2, c=16)
+        s_view = stage1[:].rearrange("p (q v h c) -> p v q h c", q=2, v=2, h=2, c=16)
+        nc.vector.tensor_tensor(out=s_view[:, 0], in0=i_view[:, 0], in1=i_view[:, 1], op=ALU.add)
+        nc.vector.tensor_tensor(
+            out=s_view[:, 1], in0=i_view[:, 0], in1=i_view[:, 1], op=ALU.subtract
+        )
+        stage2 = const.tile([P, P], F32)
+        e_view = stage1[:].rearrange("p (w r e) -> p e w r", r=32, e=2)
+        h_view = stage2[:].rearrange("p (w h r) -> p h w r", h=2, r=32)
+        nc.vector.tensor_tensor(out=h_view[:, 0], in0=e_view[:, 0], in1=e_view[:, 1], op=ALU.add)
+        nc.vector.tensor_tensor(
+            out=h_view[:, 1], in0=e_view[:, 0], in1=e_view[:, 1], op=ALU.subtract
+        )
+        haar = const.tile([P, P], BF16)
+        nc.vector.tensor_scalar_mul(out=haar[:], in0=stage2[:], scalar1=0.5)
+
+        grouped = {
+            "add": const.tile([P, PASSES, N_ADD * BANK], BF16, align_bytes=64, name="grouped_add"),
+            "mm": const.tile([P, PASSES, N_MM * BANK], BF16, align_bytes=64, name="grouped_mm"),
+        }
+        w_sorted = {}
+        w_grouped = {}
+        w_mx = {}
+        finish_order = [("mm", r) for r in range(N_MM)] + [("add", r) for r in range(N_ADD)]
+
+        for k in range(FRAMES + 1):
+            here = k < FRAMES
+            behind = k >= 1
+
+            def finish(a):
+                if behind:
+                    for way, r in finish_order[a : a + 2]:
+                        multiply(k - 1, way, r)
+                    for way, r in finish_order[a : a + 2]:
+                        add_bias(k - 1, way, r)
+                else:
+                    way = "add" if a < 4 else "mm"
+                    turn_w(way, a % 4)
+                    turn_w(way, a % 4 + 1)
+                    if a == 2:
+                        sort_w("mm")
                     if a % 4 == 2:
-                        w_quantise(kind)
+                        quantise_w(way)
 
-            def start_g(u):
-                if cur:
-                    t_g(k, u)
-                    e_copy(k, u)
+            if behind:
+                vertical(k + 1, nc.gpsimd, [(0, N_ADD)])
 
-            def start_p(p):
-                if cur:
-                    t_p(k, p)
-                    x_copy(k, p)
-
-            def mid_p(p):
-                if cur:
-                    haar_mm(k, p)
-                    g_copy(k, p)
-
-            def end_g(u):
-                if cur:
-                    horizontal(k, u)
-
-            start_g(0)
-            start_p(0)
-            if 2 <= k <= K:
-                store(k - 2, "G", 0, NG)
-            end_g(0)
-            finish(0, 2)
-            start_g(1)
-            mid_p(0)
-            start_p(1)
-            end_g(1)
-            finish(2, 4)
-            start_g(2)
-            mid_p(1)
-            start_p(2)
-            end_g(2)
-            finish(4, 6)
-            if prv:
-                store(k - 1, "P", 0, NP)
-            if k == K:
-                store(k - 1, "G", 0, 3)
-            start_g(3)
-            mid_p(2)
-            end_g(3)
-            if cur:
-                q_kind(k, "P", [(0, 256), (256, 384)])
-                q_kind(k, "G", [(0, 512)])
-            finish(6, 8)
-            if k == K:
-                store(k - 1, "G", 3, NG)
-            start_g(4)
-            pre_permute(k + 1)
-            end_g(4)
-            if cur:
-                q_kind(k, "G", [(512, 640)])
+            if here:
+                turn_add(k, 0)
+            if k == 0:
+                sort_w("add")
+                gather_blocks(0)
+            if here:
+                turn_mm(k, 0)
+            load(k + AHEAD, [(0, N_ADD)])
+            load_mm(k + AHEAD)
+            if 2 <= k:
+                store(k - 2, "add", 0, N_ADD)
+            if here:
+                horizontal(k, 0)
+            if behind:
+                quantise_t(k - 1, "add", 4 * P, 5 * P)
+            finish(0)
+            if here:
+                turn_add(k, 1)
+                haar_mm(k, 0)
+                turn_mm(k, 1)
+                horizontal(k, 1)
+            finish(2)
+            if here:
+                turn_add(k, 2)
+                haar_mm(k, 1)
+                turn_mm(k, 2)
+                horizontal(k, 2)
+            finish(4)
+            if behind:
+                store(k - 1, "mm", 0, N_MM)
+            if here:
+                turn_add(k, 3)
+                haar_mm(k, 2)
+                horizontal(k, 3)
+                quantise_t(k, "mm", 0, 2 * P)
+                quantise_t(k, "mm", 2 * P, 3 * P)
+                quantise_t(k, "add", 0, 4 * P)
+            else:
+                store(k - 1, "add", 0, 3)
+            finish(6)
+            if here:
+                turn_add(k, 4)
+                gather_blocks(k + 1)
+                horizontal(k, 4)
+            else:
+                store(k - 1, "add", 3, N_ADD)

@@ -33,6 +33,7 @@ def tile_waveletlinearlayer_t_kernel(tc, x, W, b, out):
         const = ctx.enter_context(tc.tile_pool(name="const", bufs=1))
         x_pool = ctx.enter_context(tc.tile_pool(name="x_pool", bufs=AHEAD))
         two = ctx.enter_context(tc.tile_pool(name="two", bufs=2))
+        one = ctx.enter_context(tc.tile_pool(name="one", bufs=1))
         psum_one = ctx.enter_context(tc.psum_pool(name="psum_one", bufs=1))
         psum_two = ctx.enter_context(tc.psum_pool(name="psum_two", bufs=2))
         ctx.enter_context(tc.manual_schedule())
@@ -106,9 +107,11 @@ def tile_waveletlinearlayer_t_kernel(tc, x, W, b, out):
             )
 
         def horizontal(k, r):
+            if r == 0:
+                live["grouped", "add", k] = new_grouped("add")
             for h in range(PASSES):
                 nc.vector.scalar_tensor_tensor(
-                    out=grouped["add"][:, h, r * BANK : (r + 1) * BANK].rearrange(
+                    out=live["grouped", "add", k][:, h, r * BANK : (r + 1) * BANK].rearrange(
                         "p (n t) -> p n t", t=SLOTS
                     ),
                     in0=live["bank", k, r, 0][:].rearrange("p (t n) -> p n t", t=SLOTS),
@@ -146,6 +149,8 @@ def tile_waveletlinearlayer_t_kernel(tc, x, W, b, out):
             nc.scalar.copy(out=x_turned[:], in_=bank[:])
 
         def haar_mm(k, r):
+            if r == 0:
+                live["grouped", "mm", k] = new_grouped("mm")
             for g in range(PASSES):
                 bank = psum_two.tile([P, BANK], F32, name="haar_out")
                 nc.tensor.matmul(
@@ -156,11 +161,15 @@ def tile_waveletlinearlayer_t_kernel(tc, x, W, b, out):
                     stop=True,
                 )
                 nc.scalar.copy(
-                    out=grouped["mm"][:, g, r * BANK : (r + 1) * BANK].rearrange(
+                    out=live["grouped", "mm", k][:, g, r * BANK : (r + 1) * BANK].rearrange(
                         "p (n t) -> p n t", t=SLOTS
                     ),
                     in_=bank[:].rearrange("p (t n) -> p n t", t=SLOTS),
                 )
+
+        def new_grouped(way):
+            n = N_ADD if way == "add" else N_MM
+            return one.tile([P, PASSES, n * BANK], BF16, align_bytes=64, name="grouped_" + way)
 
         def quantise(values, codes, scales, a, z):
             for g in range(PASSES):
@@ -178,7 +187,7 @@ def tile_waveletlinearlayer_t_kernel(tc, x, W, b, out):
                     two.tile([P, PASSES, n * P], U8, align_bytes=64, name="scales_" + way),
                 )
             codes, scales = live["codes", way, k]
-            quantise(grouped[way], codes, scales, a, z)
+            quantise(live["grouped", way, k], codes, scales, a, z)
 
         def multiply(k, way, r):
             codes, scales = live["codes", way, k]
@@ -209,12 +218,9 @@ def tile_waveletlinearlayer_t_kernel(tc, x, W, b, out):
                 op=ALU.add,
             )
 
-        def store(k, way, a, z):
-            first = 0 if way == "add" else N_ADD
-            nc.scalar.dma_start(
-                out=frame_rows(out, k)[:, first + a : first + z, :],
-                in_=live["result", way, k][:, a:z, :],
-            )
+        def store(k, way):
+            a, z = (0, N_ADD) if way == "add" else (N_ADD, N_TILES)
+            nc.scalar.dma_start(out=frame_rows(out, k)[:, a:z, :], in_=live["result", way, k][:])
 
         def sort_w(way):
             w_sorted[way] = const.tile([P, 2 * FEAT], F32, name="w_sorted_" + way)
@@ -240,7 +246,8 @@ def tile_waveletlinearlayer_t_kernel(tc, x, W, b, out):
                 w_grouped[way] = two.tile(
                     [P, PASSES, SLOTS * OUT], BF16, tag="result_add", align_bytes=64, name="w_grouped"
                 )
-            pool, tag = ((psum_one, "turned"), (psum_two, "haar_out"))[a % 2]
+            turn = (a if way == "add" else a + 4) % 3
+            pool, tag = ((psum_one, "turned"), (psum_two, "haar_out"), (psum_two, "haar_out"))[turn]
             bank = eight_transposes(w_sorted[way][:].bitcast(BF16), 4, a, pool, tag)
             dst = w_grouped[way][:, :, a * BANK : (a + 1) * BANK].rearrange(
                 "p g (n t) -> p g n t", t=SLOTS
@@ -298,18 +305,18 @@ def tile_waveletlinearlayer_t_kernel(tc, x, W, b, out):
         haar = const.tile([P, P], BF16)
         nc.vector.tensor_scalar_mul(out=haar[:], in0=stage2[:], scalar1=0.5)
 
-        grouped = {
-            "add": const.tile([P, PASSES, N_ADD * BANK], BF16, align_bytes=64, name="grouped_add"),
-            "mm": const.tile([P, PASSES, N_MM * BANK], BF16, align_bytes=64, name="grouped_mm"),
-        }
         w_sorted = {}
         w_grouped = {}
         w_mx = {}
         finish_order = [("mm", r) for r in range(N_MM)] + [("add", r) for r in range(N_ADD)]
 
-        for k in range(FRAMES + 1):
+        sort_w("add")
+        gather_blocks(0)
+        sort_w("mm")
+
+        for k in range(FRAMES + 2):
             here = k < FRAMES
-            behind = k >= 1
+            behind = 1 <= k <= FRAMES
 
             def finish(a):
                 if behind:
@@ -317,33 +324,25 @@ def tile_waveletlinearlayer_t_kernel(tc, x, W, b, out):
                         multiply(k - 1, way, r)
                     for way, r in finish_order[a : a + 2]:
                         add_bias(k - 1, way, r)
-                else:
+                if k == 0:
                     way = "add" if a < 4 else "mm"
                     turn_w(way, a % 4)
                     turn_w(way, a % 4 + 1)
-                    if a == 2:
-                        sort_w("mm")
                     if a % 4 == 2:
                         quantise_w(way)
 
-            if behind:
+            load(k + AHEAD, [(0, N_ADD)])
+            load_mm(k + AHEAD)
+            if k >= 1:
                 vertical(k + 1, nc.gpsimd, [(0, N_ADD)])
 
             if here:
                 turn_add(k, 0)
-            if k == 0:
-                sort_w("add")
-                gather_blocks(0)
-            if here:
                 turn_mm(k, 0)
-            load(k + AHEAD, [(0, N_ADD)])
-            load_mm(k + AHEAD)
-            if 2 <= k:
-                store(k - 2, "add", 0, N_ADD)
+            if k >= 2:
+                store(k - 2, "add")
             if here:
                 horizontal(k, 0)
-            if behind:
-                quantise_t(k - 1, "add", 4 * P, 5 * P)
             finish(0)
             if here:
                 turn_add(k, 1)
@@ -358,20 +357,17 @@ def tile_waveletlinearlayer_t_kernel(tc, x, W, b, out):
                 horizontal(k, 2)
             finish(4)
             if behind:
-                store(k - 1, "mm", 0, N_MM)
+                store(k - 1, "mm")
             if here:
                 turn_add(k, 3)
                 haar_mm(k, 2)
                 horizontal(k, 3)
                 quantise_t(k, "mm", 0, 2 * P)
                 quantise_t(k, "mm", 2 * P, 3 * P)
-                quantise_t(k, "add", 0, 4 * P)
-            else:
-                store(k - 1, "add", 0, 3)
             finish(6)
             if here:
                 turn_add(k, 4)
                 gather_blocks(k + 1)
                 horizontal(k, 4)
-            else:
-                store(k - 1, "add", 3, N_ADD)
+                quantise_t(k, "add", 0, 4 * P)
+                quantise_t(k, "add", 4 * P, 5 * P)

@@ -32,10 +32,10 @@ def tile_waveletlinearlayer_t_kernel(tc, x, W, b, out):
     with ExitStack() as ctx:
         const = ctx.enter_context(tc.tile_pool(name="const", bufs=1))
         x_pool = ctx.enter_context(tc.tile_pool(name="x_pool", bufs=AHEAD))
-        two = ctx.enter_context(tc.tile_pool(name="two", bufs=2))
-        one = ctx.enter_context(tc.tile_pool(name="one", bufs=1))
-        psum_one = ctx.enter_context(tc.psum_pool(name="psum_one", bufs=1))
-        psum_two = ctx.enter_context(tc.psum_pool(name="psum_two", bufs=2))
+        ring = ctx.enter_context(tc.tile_pool(name="ring", bufs=2))
+        single = ctx.enter_context(tc.tile_pool(name="single", bufs=1))
+        psum_single = ctx.enter_context(tc.psum_pool(name="psum_single", bufs=1))
+        psum_ring = ctx.enter_context(tc.psum_pool(name="psum_ring", bufs=2))
         ctx.enter_context(tc.manual_schedule())
 
         live = {}
@@ -43,43 +43,43 @@ def tile_waveletlinearlayer_t_kernel(tc, x, W, b, out):
         def frame_rows(ap, k):
             return ap[k * FRAME : (k + 1) * FRAME, :].rearrange("(p r) f -> p r f", r=N_TILES)
 
-        def load(k, cuts):
+        def load_add(k, cuts):
             if k >= FRAMES:
                 return
             x_add = x_pool.tile([P, N_ADD * FEAT], BF16, name="x_add")
-            x_mm = x_pool.tile([P, N_MM * FEAT], BF16, name="x_mm")
             live["x_add", k] = x_add
-            live["x_mm", k] = x_mm
-            for a, z in cuts:
+            for lo, hi in cuts:
                 nc.sync.dma_start(
-                    out=x_add[:, a * FEAT : z * FEAT].rearrange("p (r f) -> p r f", f=FEAT),
-                    in_=frame_rows(x, k)[:, a:z, :],
+                    out=x_add[:, lo * FEAT : hi * FEAT].rearrange("p (r f) -> p r f", f=FEAT),
+                    in_=frame_rows(x, k)[:, lo:hi, :],
                 )
 
         def load_mm(k):
             if k >= FRAMES:
                 return
+            x_mm = x_pool.tile([P, N_MM * FEAT], BF16, name="x_mm")
+            live["x_mm", k] = x_mm
             nc.sync.dma_start(
-                out=live["x_mm", k][:].rearrange("p (r f) -> p r f", f=FEAT),
+                out=x_mm[:].rearrange("p (r f) -> p r f", f=FEAT),
                 in_=frame_rows(x, k)[:, N_ADD:N_TILES, :],
             )
 
         def vertical(k, engine, cuts):
             if k >= FRAMES:
                 return
-            u = two.tile([P, N_ADD * FEAT], F32, name="u")
-            live["u", k] = u
-            u_view = u[:].rearrange(
-                "p (e t q v h j) -> p e v t q h j", e=2, t=4, q=4 * N_ADD, v=2, h=2, j=8
+            vert = ring.tile([P, N_ADD * FEAT], F32, name="vert")
+            live["vert", k] = vert
+            vert_view = vert[:].rearrange(
+                "p (e t q v y j) -> p e v t q y j", e=2, t=4, q=4 * N_ADD, v=2, y=2, j=8
             )
-            for a, z in cuts:
-                x_view = live["x_add", k][:, a * FEAT : z * FEAT].rearrange(
-                    "p (q h t s j e) -> p s e t q h j", q=4 * (z - a), h=2, t=4, s=2, j=8, e=2
+            for lo, hi in cuts:
+                x_view = live["x_add", k][:, lo * FEAT : hi * FEAT].rearrange(
+                    "p (q y t s j e) -> p s e t q y j", q=4 * (hi - lo), y=2, t=4, s=2, j=8, e=2
                 )
                 for e in (1, 0):
                     for v in range(2):
                         engine.tensor_tensor(
-                            out=u_view[:, e, v, :, 4 * a : 4 * z],
+                            out=vert_view[:, e, v, :, 4 * lo : 4 * hi],
                             in0=x_view[:, 0, e],
                             in1=x_view[:, 1, e],
                             op=(ALU.add if v == 0 else ALU.subtract),
@@ -88,16 +88,16 @@ def tile_waveletlinearlayer_t_kernel(tc, x, W, b, out):
         def turn_add(k, r):
             for e in (1, 0):
                 if e == 1:
-                    bank = psum_one.tile([P, BANK], F32, name="odd")
+                    bank = psum_single.tile([P, BANK], F32, name="odd")
                 else:
-                    bank = psum_two.tile([P, BANK], F32, name="even")
+                    bank = psum_ring.tile([P, BANK], F32, name="even")
                 live["bank", k, r, e] = bank
                 for t in range(SLOTS):
                     c0 = e * (N_ADD * BANK) + t * (N_ADD * P) + r * P
                     nc.tensor.transpose(
-                        bank[:, t * P : (t + 1) * P], live["u", k][:, c0 : c0 + P], ident_f32[:]
+                        bank[:, t * P : (t + 1) * P], live["vert", k][:, c0 : c0 + P], ident_f32[:]
                     )
-            odd_half = two.tile([P, P, SLOTS], F32, name="odd_half")
+            odd_half = ring.tile([P, P, SLOTS], F32, name="odd_half")
             live["odd_half", k, r] = odd_half
             nc.scalar.activation(
                 out=odd_half[:],
@@ -124,13 +124,13 @@ def tile_waveletlinearlayer_t_kernel(tc, x, W, b, out):
         def gather_blocks(k):
             if k >= FRAMES:
                 return
-            x_sorted = two.tile([P, N_MM * FEAT // 2], F32, name="x_sorted")
+            x_sorted = ring.tile([P, N_MM * FEAT // 2], F32, name="x_sorted")
             live["x_sorted", k] = x_sorted
             nc.scalar.copy(
-                out=x_sorted[:].rearrange("p (t m c) -> p t m c", t=4, m=8 * N_MM, c=16),
+                out=x_sorted[:].rearrange("p (t m w) -> p t m w", t=4, m=8 * N_MM, w=16),
                 in_=live["x_mm", k][:]
                 .bitcast(F32)
-                .rearrange("p (m t c) -> p t m c", m=8 * N_MM, t=4, c=16),
+                .rearrange("p (m t w) -> p t m w", m=8 * N_MM, t=4, w=16),
             )
 
         def eight_transposes(src, row_tiles, r, pool, tag):
@@ -143,8 +143,10 @@ def tile_waveletlinearlayer_t_kernel(tc, x, W, b, out):
             return bank
 
         def turn_mm(k, r):
-            bank = eight_transposes(live["x_sorted", k][:].bitcast(BF16), N_MM, r, psum_one, "turned")
-            x_turned = two.tile([P, PASSES * SLOTS * P], BF16, name="x_turned")
+            bank = eight_transposes(
+                live["x_sorted", k][:].bitcast(BF16), N_MM, r, psum_single, "turned"
+            )
+            x_turned = ring.tile([P, PASSES * SLOTS * P], BF16, name="x_turned")
             live["x_turned", k, r] = x_turned
             nc.scalar.copy(out=x_turned[:], in_=bank[:])
 
@@ -152,7 +154,7 @@ def tile_waveletlinearlayer_t_kernel(tc, x, W, b, out):
             if r == 0:
                 live["grouped", "mm", k] = new_grouped("mm")
             for g in range(PASSES):
-                bank = psum_two.tile([P, BANK], F32, name="haar_out")
+                bank = psum_ring.tile([P, BANK], F32, name="haar_out")
                 nc.tensor.matmul(
                     out=bank[:],
                     lhsT=haar[:],
@@ -168,31 +170,33 @@ def tile_waveletlinearlayer_t_kernel(tc, x, W, b, out):
                 )
 
         def new_grouped(way):
-            n = N_ADD if way == "add" else N_MM
-            return one.tile([P, PASSES, n * BANK], BF16, align_bytes=64, name="grouped_" + way)
+            n_tiles = N_ADD if way == "add" else N_MM
+            return single.tile(
+                [P, PASSES, n_tiles * BANK], BF16, align_bytes=64, name="grouped_" + way
+            )
 
-        def quantise(values, codes, scales, a, z):
+        def quantise(values, codes, scales, lo, hi):
             for g in range(PASSES):
                 nc.vector.quantize_mx(
-                    out=codes[:, g, a:z].bitcast(FP8X4),
-                    scales=scales[:, g, a:z],
-                    in_=values[:, g, SLOTS * a : SLOTS * z],
+                    out=codes[:, g, lo:hi].bitcast(FP8X4),
+                    scales=scales[:, g, lo:hi],
+                    in_=values[:, g, SLOTS * lo : SLOTS * hi],
                 )
 
-        def quantise_t(k, way, a, z):
-            if a == 0:
-                n = N_ADD if way == "add" else N_MM
+        def quantise_t(k, way, lo, hi):
+            if lo == 0:
+                n_tiles = N_ADD if way == "add" else N_MM
                 live["codes", way, k] = (
-                    two.tile([P, PASSES, n * P], U32, align_bytes=64, name="codes_" + way),
-                    two.tile([P, PASSES, n * P], U8, align_bytes=64, name="scales_" + way),
+                    ring.tile([P, PASSES, n_tiles * P], U32, align_bytes=64, name="codes_" + way),
+                    ring.tile([P, PASSES, n_tiles * P], U8, align_bytes=64, name="scales_" + way),
                 )
             codes, scales = live["codes", way, k]
-            quantise(live["grouped", way, k], codes, scales, a, z)
+            quantise(live["grouped", way, k], codes, scales, lo * P, hi * P)
 
         def multiply(k, way, r):
             codes, scales = live["codes", way, k]
             w_codes, w_scales = w_mx[way]
-            acc = psum_two.tile([P, OUT], F32, name="acc")
+            acc = psum_ring.tile([P, OUT], F32, name="acc")
             live["acc", k, way, r] = acc
             for g in range(PASSES):
                 nc.tensor.matmul_mx(
@@ -207,9 +211,9 @@ def tile_waveletlinearlayer_t_kernel(tc, x, W, b, out):
 
         def add_bias(k, way, r):
             if r == 0:
-                n = N_ADD if way == "add" else N_MM
-                live["result", way, k] = two.tile(
-                    [P, n, OUT], F32, tag="result_" + way, align_bytes=64, name="result"
+                n_tiles = N_ADD if way == "add" else N_MM
+                live["result", way, k] = ring.tile(
+                    [P, n_tiles, OUT], F32, tag="result_" + way, align_bytes=64, name="result"
                 )
             nc.vector.tensor_tensor(
                 out=live["result", way, k][:, r, :],
@@ -218,38 +222,45 @@ def tile_waveletlinearlayer_t_kernel(tc, x, W, b, out):
                 op=ALU.add,
             )
 
-        def store(k, way):
-            a, z = (0, N_ADD) if way == "add" else (N_ADD, N_TILES)
-            nc.scalar.dma_start(out=frame_rows(out, k)[:, a:z, :], in_=live["result", way, k][:])
+        def store(k, way, lo, hi):
+            first = 0 if way == "add" else N_ADD
+            nc.scalar.dma_start(
+                out=frame_rows(out, k)[:, first + lo : first + hi, :],
+                in_=live["result", way, k][:, lo:hi, :],
+            )
 
         def sort_w(way):
             w_sorted[way] = const.tile([P, 2 * FEAT], F32, name="w_sorted_" + way)
             words = w_rows[:].bitcast(F32)
             if way == "add":
                 dst = w_sorted[way][:].rearrange(
-                    "p (t a h c r j) -> p t h a c r j", t=4, a=4, h=2, c=4, r=4, j=4
+                    "p (t o h c z j) -> p t h o c z j", t=4, o=4, h=2, c=4, z=4, j=4
                 )
                 src = words.rearrange(
-                    "p (a c h r t j) -> p t h a c r j", a=4, c=4, h=2, r=4, t=4, j=4
+                    "p (o c h z t j) -> p t h o c z j", o=4, c=4, h=2, z=4, t=4, j=4
                 )
                 for t in range(SLOTS):
                     for h in range(PASSES):
                         nc.scalar.copy(out=dst[:, t, h], in_=src[:, t, h])
             else:
-                dst = w_sorted[way][:].rearrange("p (t a m j) -> p t a m j", t=4, a=4, m=32, j=4)
-                src = words.rearrange("p (a m t j) -> p t a m j", a=4, m=32, t=4, j=4)
+                dst = w_sorted[way][:].rearrange("p (t o m j) -> p t o m j", t=4, o=4, m=32, j=4)
+                src = words.rearrange("p (o m t j) -> p t o m j", o=4, m=32, t=4, j=4)
                 for t in range(SLOTS):
                     nc.scalar.copy(out=dst[:, t], in_=src[:, t])
 
-        def turn_w(way, a):
-            if a == 0:
-                w_grouped[way] = two.tile(
+        def turn_w(way, o):
+            if o == 0:
+                w_grouped[way] = ring.tile(
                     [P, PASSES, SLOTS * OUT], BF16, tag="result_add", align_bytes=64, name="w_grouped"
                 )
-            turn = (a if way == "add" else a + 4) % 3
-            pool, tag = ((psum_one, "turned"), (psum_two, "haar_out"), (psum_two, "haar_out"))[turn]
-            bank = eight_transposes(w_sorted[way][:].bitcast(BF16), 4, a, pool, tag)
-            dst = w_grouped[way][:, :, a * BANK : (a + 1) * BANK].rearrange(
+            turn = (o if way == "add" else o + 4) % 3
+            pool, tag = (
+                (psum_single, "turned"),
+                (psum_ring, "haar_out"),
+                (psum_ring, "haar_out"),
+            )[turn]
+            bank = eight_transposes(w_sorted[way][:].bitcast(BF16), 4, o, pool, tag)
+            dst = w_grouped[way][:, :, o * BANK : (o + 1) * BANK].rearrange(
                 "p g (n t) -> p g n t", t=SLOTS
             )
             src = bank[:].rearrange("p (g t n) -> p g n t", g=PASSES, t=SLOTS)
@@ -265,19 +276,21 @@ def tile_waveletlinearlayer_t_kernel(tc, x, W, b, out):
             )
             quantise(w_grouped[way], w_mx[way][0], w_mx[way][1], 0, OUT)
 
-        load(0, [(0, 2), (2, N_ADD)])
+        first_cuts = [(0, 2), (2, N_ADD)]
+        whole = [(0, N_ADD)]
+        load_add(0, first_cuts)
         w_rows = const.tile([P, 4 * FEAT], BF16)
         nc.sync.dma_start(
-            out=w_rows[:].rearrange("p (a f) -> p a f", f=FEAT),
-            in_=W.rearrange("(a p) f -> p a f", p=P),
+            out=w_rows[:].rearrange("p (o f) -> p o f", f=FEAT),
+            in_=W.rearrange("(o p) f -> p o f", p=P),
         )
         load_mm(0)
-        load(1, [(0, N_ADD)])
+        load_add(1, whole)
         bias = const.tile([P, OUT], BF16)
         nc.sync.dma_start(out=bias[:], in_=b.partition_broadcast(P))
         load_mm(1)
         for k in range(2, AHEAD):
-            load(k, [(0, N_ADD)])
+            load_add(k, whole)
             load_mm(k)
 
         ident = const.tile([P, P], BF16)
@@ -285,19 +298,19 @@ def tile_waveletlinearlayer_t_kernel(tc, x, W, b, out):
         ident_f32 = const.tile([P, P], F32)
         make_identity(nc, ident_f32[:])
 
-        vertical(0, nc.vector, [(0, 2), (2, N_ADD)])
-        vertical(1, nc.gpsimd, [(0, N_ADD)])
+        vertical(0, nc.vector, first_cuts)
+        vertical(1, nc.gpsimd, whole)
 
         stage1 = const.tile([P, P], F32)
-        i_view = ident[:].rearrange("p (q h s c) -> p s q h c", q=2, h=2, s=2, c=16)
-        s_view = stage1[:].rearrange("p (q v h c) -> p v q h c", q=2, v=2, h=2, c=16)
+        i_view = ident[:].rearrange("p (d y s l) -> p s d y l", d=2, y=2, s=2, l=16)
+        s_view = stage1[:].rearrange("p (d v y l) -> p v d y l", d=2, v=2, y=2, l=16)
         nc.vector.tensor_tensor(out=s_view[:, 0], in0=i_view[:, 0], in1=i_view[:, 1], op=ALU.add)
         nc.vector.tensor_tensor(
             out=s_view[:, 1], in0=i_view[:, 0], in1=i_view[:, 1], op=ALU.subtract
         )
         stage2 = const.tile([P, P], F32)
-        e_view = stage1[:].rearrange("p (w r e) -> p e w r", r=32, e=2)
-        h_view = stage2[:].rearrange("p (w h r) -> p h w r", h=2, r=32)
+        e_view = stage1[:].rearrange("p (d m e) -> p e d m", m=32, e=2)
+        h_view = stage2[:].rearrange("p (d h m) -> p h d m", h=2, m=32)
         nc.vector.tensor_tensor(out=h_view[:, 0], in0=e_view[:, 0], in1=e_view[:, 1], op=ALU.add)
         nc.vector.tensor_tensor(
             out=h_view[:, 1], in0=e_view[:, 0], in1=e_view[:, 1], op=ALU.subtract
@@ -310,37 +323,39 @@ def tile_waveletlinearlayer_t_kernel(tc, x, W, b, out):
         w_mx = {}
         finish_order = [("mm", r) for r in range(N_MM)] + [("add", r) for r in range(N_ADD)]
 
-        sort_w("add")
-        gather_blocks(0)
-        sort_w("mm")
-
-        for k in range(FRAMES + 2):
+        for k in range(FRAMES + 1):
             here = k < FRAMES
-            behind = 1 <= k <= FRAMES
+            behind = k >= 1
 
-            def finish(a):
+            def finish(first):
                 if behind:
-                    for way, r in finish_order[a : a + 2]:
+                    for way, r in finish_order[first : first + 2]:
                         multiply(k - 1, way, r)
-                    for way, r in finish_order[a : a + 2]:
+                    for way, r in finish_order[first : first + 2]:
                         add_bias(k - 1, way, r)
-                if k == 0:
-                    way = "add" if a < 4 else "mm"
-                    turn_w(way, a % 4)
-                    turn_w(way, a % 4 + 1)
-                    if a % 4 == 2:
+                else:
+                    way = "add" if first < 4 else "mm"
+                    turn_w(way, first % 4)
+                    turn_w(way, first % 4 + 1)
+                    if first == 2:
+                        sort_w("mm")
+                    if first % 4 == 2:
                         quantise_w(way)
 
-            load(k + AHEAD, [(0, N_ADD)])
-            load_mm(k + AHEAD)
-            if k >= 1:
-                vertical(k + 1, nc.gpsimd, [(0, N_ADD)])
+            if behind:
+                vertical(k + 1, nc.gpsimd, whole)
 
             if here:
                 turn_add(k, 0)
+            if k == 0:
+                sort_w("add")
+                gather_blocks(0)
+            if here:
                 turn_mm(k, 0)
+            load_add(k + AHEAD, whole)
+            load_mm(k + AHEAD)
             if k >= 2:
-                store(k - 2, "add")
+                store(k - 2, "add", 0, N_ADD)
             if here:
                 horizontal(k, 0)
             finish(0)
@@ -357,17 +372,21 @@ def tile_waveletlinearlayer_t_kernel(tc, x, W, b, out):
                 horizontal(k, 2)
             finish(4)
             if behind:
-                store(k - 1, "mm")
+                store(k - 1, "mm", 0, N_MM)
             if here:
                 turn_add(k, 3)
                 haar_mm(k, 2)
                 horizontal(k, 3)
-                quantise_t(k, "mm", 0, 2 * P)
-                quantise_t(k, "mm", 2 * P, 3 * P)
+                quantise_t(k, "mm", 0, 2)
+                quantise_t(k, "mm", 2, 3)
+            else:
+                store(k - 1, "add", 0, 3)
             finish(6)
             if here:
                 turn_add(k, 4)
                 gather_blocks(k + 1)
                 horizontal(k, 4)
-                quantise_t(k, "add", 0, 4 * P)
-                quantise_t(k, "add", 4 * P, 5 * P)
+                quantise_t(k, "add", 0, 4)
+                quantise_t(k, "add", 4, 5)
+            else:
+                store(k - 1, "add", 3, N_ADD)

@@ -19,118 +19,119 @@ OUT = 512
 SLOTS = 4
 PASSES = 2
 BANK = 512
-N_ADD = 5
-N_MM = 3
-N_TILES = N_ADD + N_MM
-FRAME = N_TILES * P
-FRAMES = 8192 // FRAME
-AHEAD = 3
+PAIR = 2
+PAIRS = 8192 // (PAIR * P)
+PERIOD = 8
+MM_PLACES = (2, 4, 7)
+
+ADD_PAIRS = [b for b in range(PAIRS) if b % PERIOD not in MM_PLACES]
+MM_PAIRS = [b for b in range(PAIRS) if b % PERIOD in MM_PLACES]
+N_ADD = PAIR * len(ADD_PAIRS)
+N_MM = PAIR * len(MM_PAIRS)
+ADD_STEP = 3
+MM_STEP = 5
+MM_START = 6
 
 
 def tile_waveletlinearlayer_t_kernel(tc, x, W, b, out):
     nc = tc.nc
     with ExitStack() as ctx:
         const = ctx.enter_context(tc.tile_pool(name="const", bufs=1))
-        x_pool = ctx.enter_context(tc.tile_pool(name="x_pool", bufs=AHEAD))
-        ring = ctx.enter_context(tc.tile_pool(name="ring", bufs=2))
-        single = ctx.enter_context(tc.tile_pool(name="single", bufs=1))
+        x_pool = ctx.enter_context(tc.tile_pool(name="x_pool", bufs=6))
+        vert_pool = ctx.enter_context(tc.tile_pool(name="vert_pool", bufs=6))
+        ring = ctx.enter_context(tc.tile_pool(name="ring", bufs=3))
         psum_single = ctx.enter_context(tc.psum_pool(name="psum_single", bufs=1))
         psum_ring = ctx.enter_context(tc.psum_pool(name="psum_ring", bufs=2))
         ctx.enter_context(tc.manual_schedule())
 
         live = {}
 
-        def frame_rows(ap, k):
-            return ap[k * FRAME : (k + 1) * FRAME, :].rearrange("(p r) f -> p r f", r=N_TILES)
+        def pair_rows(ap, way, i):
+            block = (ADD_PAIRS if way == "add" else MM_PAIRS)[i]
+            rows = PAIR * P
+            return ap[block * rows : (block + 1) * rows, :].rearrange("(p r) f -> p r f", r=PAIR)
 
-        def load_add(k, cuts):
-            if k >= FRAMES:
-                return
-            x_add = x_pool.tile([P, N_ADD * FEAT], BF16, name="x_add")
-            live["x_add", k] = x_add
-            for lo, hi in cuts:
-                nc.sync.dma_start(
-                    out=x_add[:, lo * FEAT : hi * FEAT].rearrange("p (r f) -> p r f", f=FEAT),
-                    in_=frame_rows(x, k)[:, lo:hi, :],
-                )
-
-        def load_mm(k):
-            if k >= FRAMES:
-                return
-            x_mm = x_pool.tile([P, N_MM * FEAT], BF16, name="x_mm")
-            live["x_mm", k] = x_mm
+        def load(way, i):
+            tile = x_pool.tile([P, PAIR * FEAT], BF16, tag="x_" + way, name="x_pair")
+            live["x", way, i] = tile
             nc.sync.dma_start(
-                out=x_mm[:].rearrange("p (r f) -> p r f", f=FEAT),
-                in_=frame_rows(x, k)[:, N_ADD:N_TILES, :],
+                out=tile[:].rearrange("p (r f) -> p r f", f=FEAT), in_=pair_rows(x, way, i)
             )
 
-        def vertical(k, engine, cuts):
-            if k >= FRAMES:
-                return
-            vert = ring.tile([P, N_ADD * FEAT], F32, name="vert")
-            live["vert", k] = vert
+        def x_tile(way, n):
+            r = n % PAIR
+            return live["x", way, n // PAIR][:, r * FEAT : (r + 1) * FEAT]
+
+        def vertical(i, engine):
+            vert = vert_pool.tile([P, PAIR * FEAT], F32, name="vert")
+            live["vert", i] = vert
             vert_view = vert[:].rearrange(
-                "p (e t q v y j) -> p e v t q y j", e=2, t=4, q=4 * N_ADD, v=2, y=2, j=8
+                "p (r e t v q j) -> p e v t r q j", r=PAIR, e=2, t=4, v=2, q=8, j=8
             )
-            for lo, hi in cuts:
-                x_view = live["x_add", k][:, lo * FEAT : hi * FEAT].rearrange(
-                    "p (q y t s j e) -> p s e t q y j", q=4 * (hi - lo), y=2, t=4, s=2, j=8, e=2
-                )
-                for e in (1, 0):
-                    for v in range(2):
-                        engine.tensor_tensor(
-                            out=vert_view[:, e, v, :, 4 * lo : 4 * hi],
-                            in0=x_view[:, 0, e],
-                            in1=x_view[:, 1, e],
-                            op=(ALU.add if v == 0 else ALU.subtract),
-                        )
-
-        def turn_add(k, r):
+            x_view = live["x", "add", i][:].rearrange(
+                "p (r q t s j e) -> p s e t r q j", r=PAIR, q=8, t=4, s=2, j=8, e=2
+            )
             for e in (1, 0):
-                if e == 1:
-                    bank = psum_single.tile([P, BANK], F32, name="odd")
-                else:
-                    bank = psum_ring.tile([P, BANK], F32, name="even")
-                live["bank", k, r, e] = bank
-                for t in range(SLOTS):
-                    c0 = e * (N_ADD * BANK) + t * (N_ADD * P) + r * P
-                    nc.tensor.transpose(
-                        bank[:, t * P : (t + 1) * P], live["vert", k][:, c0 : c0 + P], ident_f32[:]
+                for v in range(2):
+                    engine.tensor_tensor(
+                        out=vert_view[:, e, v],
+                        in0=x_view[:, 0, e],
+                        in1=x_view[:, 1, e],
+                        op=(ALU.add if v == 0 else ALU.subtract),
                     )
+
+        def turn_add(n, e):
+            if e == 1:
+                bank = psum_single.tile([P, BANK], F32, name="odd")
+            else:
+                bank = psum_ring.tile([P, BANK], F32, name="even")
+            live["bank", n, e] = bank
+            for t in range(SLOTS):
+                c0 = (n % PAIR) * FEAT + (e * SLOTS + t) * P
+                nc.tensor.transpose(
+                    bank[:, t * P : (t + 1) * P],
+                    live["vert", n // PAIR][:, c0 : c0 + P],
+                    ident_f32[:],
+                )
+
+        def halve_odd(n):
             odd_half = ring.tile([P, P, SLOTS], F32, name="odd_half")
-            live["odd_half", k, r] = odd_half
+            live["odd_half", n] = odd_half
             nc.scalar.activation(
                 out=odd_half[:],
-                in_=live["bank", k, r, 1][:].rearrange("p (t n) -> p n t", t=SLOTS),
+                in_=live["bank", n, 1][:].rearrange("p (t n) -> p n t", t=SLOTS),
                 func=ACT.Copy,
                 scale=0.5,
             )
 
-        def horizontal(k, r):
-            if r == 0:
-                live["grouped", "add", k] = new_grouped("add")
+        def grouped_view(way, n, g):
+            r = n % PAIR
+            if r == 0 and g == 0:
+                live["grouped", way, n // PAIR] = ring.tile(
+                    [P, PAIR * PASSES * BANK], BF16, align_bytes=64, tag="grouped_" + way, name="grouped"
+                )
+            c0 = (r * PASSES + g) * BANK
+            return live["grouped", way, n // PAIR][:, c0 : c0 + BANK].rearrange(
+                "p (n t) -> p n t", t=SLOTS
+            )
+
+        def horizontal(n):
             for h in range(PASSES):
                 nc.vector.scalar_tensor_tensor(
-                    out=live["grouped", "add", k][:, h, r * BANK : (r + 1) * BANK].rearrange(
-                        "p (n t) -> p n t", t=SLOTS
-                    ),
-                    in0=live["bank", k, r, 0][:].rearrange("p (t n) -> p n t", t=SLOTS),
+                    out=grouped_view("add", n, h),
+                    in0=live["bank", n, 0][:].rearrange("p (t n) -> p n t", t=SLOTS),
                     scalar=0.5,
-                    in1=live["odd_half", k, r][:],
+                    in1=live["odd_half", n][:],
                     op0=ALU.mult,
                     op1=(ALU.add if h == 0 else ALU.subtract),
                 )
 
-        def gather_blocks(k):
-            if k >= FRAMES:
-                return
-            x_sorted = ring.tile([P, N_MM * FEAT // 2], F32, name="x_sorted")
-            live["x_sorted", k] = x_sorted
+        def gather_blocks(n):
+            x_sorted = ring.tile([P, FEAT // 2], F32, name="x_sorted")
+            live["x_sorted", n] = x_sorted
             nc.scalar.copy(
-                out=x_sorted[:].rearrange("p (t m w) -> p t m w", t=4, m=8 * N_MM, w=16),
-                in_=live["x_mm", k][:]
-                .bitcast(F32)
-                .rearrange("p (m t w) -> p t m w", m=8 * N_MM, t=4, w=16),
+                out=x_sorted[:].rearrange("p (t m w) -> p t m w", t=4, m=8, w=16),
+                in_=x_tile("mm", n).bitcast(F32).rearrange("p (m t w) -> p t m w", m=8, t=4, w=16),
             )
 
         def eight_transposes(src, row_tiles, r, pool, tag):
@@ -142,106 +143,89 @@ def tile_waveletlinearlayer_t_kernel(tc, x, W, b, out):
                     nc.tensor.transpose(bank[:, c1 : c1 + P], src[:, c0 : c0 + P], ident[:])
             return bank
 
-        def turn_mm(k, r):
-            bank = eight_transposes(
-                live["x_sorted", k][:].bitcast(BF16), N_MM, r, psum_single, "turned"
+        def turn_mm(n):
+            live["turned", n] = eight_transposes(
+                live["x_sorted", n][:].bitcast(BF16), 1, 0, psum_single, "turned"
             )
+
+        def copy_turned(n):
+            bank = live["turned", n]
             x_turned = ring.tile([P, PASSES * SLOTS * P], BF16, name="x_turned")
-            live["x_turned", k, r] = x_turned
+            live["x_turned", n] = x_turned
             nc.scalar.copy(out=x_turned[:], in_=bank[:])
 
-        def haar_mm(k, r):
-            if r == 0:
-                live["grouped", "mm", k] = new_grouped("mm")
+        def haar_mm(n):
             for g in range(PASSES):
                 bank = psum_ring.tile([P, BANK], F32, name="haar_out")
+                live["haar_out", n, g] = bank
                 nc.tensor.matmul(
                     out=bank[:],
                     lhsT=haar[:],
-                    rhs=live["x_turned", k, r][:, g * BANK : (g + 1) * BANK],
+                    rhs=live["x_turned", n][:, g * BANK : (g + 1) * BANK],
                     start=True,
                     stop=True,
                 )
+
+        def copy_haar(n):
+            for g in range(PASSES):
                 nc.scalar.copy(
-                    out=live["grouped", "mm", k][:, g, r * BANK : (r + 1) * BANK].rearrange(
-                        "p (n t) -> p n t", t=SLOTS
-                    ),
-                    in_=bank[:].rearrange("p (t n) -> p n t", t=SLOTS),
+                    out=grouped_view("mm", n, g),
+                    in_=live["haar_out", n, g][:].rearrange("p (t n) -> p n t", t=SLOTS),
                 )
 
-        def new_grouped(way):
-            n_tiles = N_ADD if way == "add" else N_MM
-            return single.tile(
-                [P, PASSES, n_tiles * BANK], BF16, align_bytes=64, name="grouped_" + way
+        def quantise(values, words, name, pool):
+            codes = pool.tile([P, words], U32, align_bytes=64, tag="codes_" + name, name="codes")
+            scales = pool.tile([P, words], U8, align_bytes=64, tag="scales_" + name, name="scales")
+            nc.vector.quantize_mx(out=codes[:].bitcast(FP8X4), scales=scales[:], in_=values)
+            return codes, scales
+
+        def quantise_t(way, i):
+            live["t", way, i] = quantise(
+                live["grouped", way, i][:], PAIR * PASSES * P, way, ring
             )
 
-        def quantise(values, codes, scales, lo, hi):
-            for g in range(PASSES):
-                nc.vector.quantize_mx(
-                    out=codes[:, g, lo:hi].bitcast(FP8X4),
-                    scales=scales[:, g, lo:hi],
-                    in_=values[:, g, SLOTS * lo : SLOTS * hi],
-                )
-
-        def quantise_t(k, way, lo, hi):
-            if lo == 0:
-                n_tiles = N_ADD if way == "add" else N_MM
-                live["codes", way, k] = (
-                    ring.tile([P, PASSES, n_tiles * P], U32, align_bytes=64, name="codes_" + way),
-                    ring.tile([P, PASSES, n_tiles * P], U8, align_bytes=64, name="scales_" + way),
-                )
-            codes, scales = live["codes", way, k]
-            quantise(live["grouped", way, k], codes, scales, lo * P, hi * P)
-
-        def multiply(k, way, r):
-            codes, scales = live["codes", way, k]
+        def multiply(way, i):
+            codes, scales = live["t", way, i]
             w_codes, w_scales = w_mx[way]
-            acc = psum_ring.tile([P, OUT], F32, name="acc")
-            live["acc", k, way, r] = acc
-            for g in range(PASSES):
-                nc.tensor.matmul_mx(
-                    out=acc[:],
-                    lhsT=codes[:, g, r * P : (r + 1) * P].bitcast(FP8X4),
-                    lhsT_scale=scales[:, g, r * P : (r + 1) * P],
-                    rhs=w_codes[:, g, :].bitcast(FP8X4),
-                    rhs_scale=w_scales[:, g, :],
-                    start=(g == 0),
-                    stop=(g == PASSES - 1),
+            for r in range(PAIR):
+                acc = psum_ring.tile([P, OUT], F32, name="acc")
+                live["acc", way, i, r] = acc
+                for g in range(PASSES):
+                    c0 = (r * PASSES + g) * P
+                    nc.tensor.matmul_mx(
+                        out=acc[:],
+                        lhsT=codes[:, c0 : c0 + P].bitcast(FP8X4),
+                        lhsT_scale=scales[:, c0 : c0 + P],
+                        rhs=w_codes[:, g * OUT : (g + 1) * OUT].bitcast(FP8X4),
+                        rhs_scale=w_scales[:, g * OUT : (g + 1) * OUT],
+                        start=(g == 0),
+                        stop=(g == PASSES - 1),
+                    )
+
+        def add_bias(way, i):
+            result = ring.tile([P, PAIR, OUT], F32, tag="result_" + way, align_bytes=64, name="result")
+            live["result", way, i] = result
+            for r in range(PAIR):
+                nc.vector.tensor_tensor(
+                    out=result[:, r, :], in0=live["acc", way, i, r][:], in1=bias[:], op=ALU.add
                 )
 
-        def add_bias(k, way, r):
-            if r == 0:
-                n_tiles = N_ADD if way == "add" else N_MM
-                live["result", way, k] = ring.tile(
-                    [P, n_tiles, OUT], F32, tag="result_" + way, align_bytes=64, name="result"
-                )
-            nc.vector.tensor_tensor(
-                out=live["result", way, k][:, r, :],
-                in0=live["acc", k, way, r][:],
-                in1=bias[:],
-                op=ALU.add,
-            )
-
-        def store(k, way, lo, hi):
-            first = 0 if way == "add" else N_ADD
-            nc.scalar.dma_start(
-                out=frame_rows(out, k)[:, first + lo : first + hi, :],
-                in_=live["result", way, k][:, lo:hi, :],
-            )
+        def store(way, i):
+            nc.sync.dma_start(out=pair_rows(out, way, i), in_=live["result", way, i][:])
 
         def sort_w(way):
             w_sorted[way] = const.tile([P, 2 * FEAT], F32, name="w_sorted_" + way)
             words = w_rows[:].bitcast(F32)
             if way == "add":
                 dst = w_sorted[way][:].rearrange(
-                    "p (t o h c z j) -> p t h o c z j", t=4, o=4, h=2, c=4, z=4, j=4
+                    "p (t o h v c y j) -> p t y o h v c j", t=4, o=4, h=2, v=2, c=4, y=2, j=4
                 )
                 src = words.rearrange(
-                    "p (o c h z t j) -> p t h o c z j", o=4, c=4, h=2, z=4, t=4, j=4
+                    "p (o c h v y t j) -> p t y o h v c j", o=4, c=4, h=2, v=2, y=2, t=4, j=4
                 )
                 for t in range(SLOTS):
-                    for h in range(PASSES):
-                        nc.scalar.copy(out=dst[:, t, h], in_=src[:, t, h])
+                    for y in range(2):
+                        nc.vector.tensor_copy(out=dst[:, t, y], in_=src[:, t, y])
             else:
                 dst = w_sorted[way][:].rearrange("p (t o m j) -> p t o m j", t=4, o=4, m=32, j=4)
                 src = words.rearrange("p (o m t j) -> p t o m j", o=4, m=32, t=4, j=4)
@@ -250,143 +234,111 @@ def tile_waveletlinearlayer_t_kernel(tc, x, W, b, out):
 
         def turn_w(way, o):
             if o == 0:
-                w_grouped[way] = ring.tile(
-                    [P, PASSES, SLOTS * OUT], BF16, tag="result_add", align_bytes=64, name="w_grouped"
+                w_grouped[way] = const.tile(
+                    [P, PASSES * SLOTS * OUT], BF16, align_bytes=64, name="w_grouped_" + way
                 )
-            turn = (o if way == "add" else o + 4) % 3
-            pool, tag = (
-                (psum_single, "turned"),
-                (psum_ring, "haar_out"),
-                (psum_ring, "haar_out"),
-            )[turn]
-            bank = eight_transposes(w_sorted[way][:].bitcast(BF16), 4, o, pool, tag)
-            dst = w_grouped[way][:, :, o * BANK : (o + 1) * BANK].rearrange(
-                "p g (n t) -> p g n t", t=SLOTS
-            )
+            bank = eight_transposes(w_sorted[way][:].bitcast(BF16), 4, o, psum_ring, "acc")
+            dst = w_grouped[way][:].rearrange("p (g m t) -> p g m t", g=PASSES, t=SLOTS)[
+                :, :, o * P : (o + 1) * P
+            ]
             src = bank[:].rearrange("p (g t n) -> p g n t", g=PASSES, t=SLOTS)
-            if way == "add":
+            if way == "add" and o % 2 == 0:
                 nc.vector.tensor_copy(out=dst, in_=src)
             else:
                 nc.scalar.copy(out=dst, in_=src)
 
         def quantise_w(way):
-            w_mx[way] = (
-                const.tile([P, PASSES, OUT], U32, align_bytes=64, name="w_codes_" + way),
-                const.tile([P, PASSES, OUT], U8, align_bytes=64, name="w_scales_" + way),
-            )
-            quantise(w_grouped[way], w_mx[way][0], w_mx[way][1], 0, OUT)
+            w_mx[way] = quantise(w_grouped[way][:], PASSES * OUT, "w_" + way, const)
 
-        first_cuts = [(0, 2), (2, N_ADD)]
-        whole = [(0, N_ADD)]
-        load_add(0, first_cuts)
         w_rows = const.tile([P, 4 * FEAT], BF16)
+        bias = const.tile([P, OUT], BF16)
+        load("add", 0)
         nc.sync.dma_start(
             out=w_rows[:].rearrange("p (o f) -> p o f", f=FEAT),
             in_=W.rearrange("(o p) f -> p o f", p=P),
         )
-        load_mm(0)
-        load_add(1, whole)
-        bias = const.tile([P, OUT], BF16)
+        load("add", 1)
+        load("mm", 0)
+        load("add", 2)
         nc.sync.dma_start(out=bias[:], in_=b.partition_broadcast(P))
-        load_mm(1)
-        for k in range(2, AHEAD):
-            load_add(k, whole)
-            load_mm(k)
+        load("mm", 1)
+        load("add", 3)
 
         ident = const.tile([P, P], BF16)
         make_identity(nc, ident[:])
         ident_f32 = const.tile([P, P], F32)
         make_identity(nc, ident_f32[:])
 
-        vertical(0, nc.vector, first_cuts)
-        vertical(1, nc.gpsimd, whole)
+        def make_haar():
+            stage1 = const.tile([P, P], F32, name="stage1")
+            i_view = ident[:].rearrange("p (d y s l) -> p s d y l", d=2, y=2, s=2, l=16)
+            s_view = stage1[:].rearrange("p (d v y l) -> p v d y l", d=2, v=2, y=2, l=16)
+            nc.vector.tensor_tensor(out=s_view[:, 0], in0=i_view[:, 0], in1=i_view[:, 1], op=ALU.add)
+            nc.vector.tensor_tensor(
+                out=s_view[:, 1], in0=i_view[:, 0], in1=i_view[:, 1], op=ALU.subtract
+            )
+            stage2 = const.tile([P, P], F32, name="stage2")
+            e_view = stage1[:].rearrange("p (d m e) -> p e d m", m=32, e=2)
+            h_view = stage2[:].rearrange("p (d h m) -> p h d m", h=2, m=32)
+            nc.vector.tensor_tensor(out=h_view[:, 0], in0=e_view[:, 0], in1=e_view[:, 1], op=ALU.add)
+            nc.vector.tensor_tensor(
+                out=h_view[:, 1], in0=e_view[:, 0], in1=e_view[:, 1], op=ALU.subtract
+            )
+            nc.vector.tensor_scalar_mul(out=haar[:], in0=stage2[:], scalar1=0.5)
 
-        stage1 = const.tile([P, P], F32)
-        i_view = ident[:].rearrange("p (d y s l) -> p s d y l", d=2, y=2, s=2, l=16)
-        s_view = stage1[:].rearrange("p (d v y l) -> p v d y l", d=2, v=2, y=2, l=16)
-        nc.vector.tensor_tensor(out=s_view[:, 0], in0=i_view[:, 0], in1=i_view[:, 1], op=ALU.add)
-        nc.vector.tensor_tensor(
-            out=s_view[:, 1], in0=i_view[:, 0], in1=i_view[:, 1], op=ALU.subtract
-        )
-        stage2 = const.tile([P, P], F32)
-        e_view = stage1[:].rearrange("p (d m e) -> p e d m", m=32, e=2)
-        h_view = stage2[:].rearrange("p (d h m) -> p h d m", h=2, m=32)
-        nc.vector.tensor_tensor(out=h_view[:, 0], in0=e_view[:, 0], in1=e_view[:, 1], op=ALU.add)
-        nc.vector.tensor_tensor(
-            out=h_view[:, 1], in0=e_view[:, 0], in1=e_view[:, 1], op=ALU.subtract
-        )
         haar = const.tile([P, P], BF16)
-        nc.vector.tensor_scalar_mul(out=haar[:], in0=stage2[:], scalar1=0.5)
-
         w_sorted = {}
         w_grouped = {}
         w_mx = {}
-        finish_order = [("mm", r) for r in range(N_MM)] + [("add", r) for r in range(N_ADD)]
 
-        for k in range(FRAMES + 1):
-            here = k < FRAMES
-            behind = k >= 1
+        def stage(start, step, count, do):
+            return (start, step, count, do)
 
-            def finish(first):
-                if behind:
-                    for way, r in finish_order[first : first + 2]:
-                        multiply(k - 1, way, r)
-                    for way, r in finish_order[first : first + 2]:
-                        add_bias(k - 1, way, r)
-                else:
-                    way = "add" if first < 4 else "mm"
-                    turn_w(way, first % 4)
-                    turn_w(way, first % 4 + 1)
-                    if first == 2:
-                        sort_w("mm")
-                    if first % 4 == 2:
-                        quantise_w(way)
-
-            if behind:
-                vertical(k + 1, nc.gpsimd, whole)
-
-            if here:
-                turn_add(k, 0)
-            if k == 0:
-                sort_w("add")
-                gather_blocks(0)
-            if here:
-                turn_mm(k, 0)
-            load_add(k + AHEAD, whole)
-            load_mm(k + AHEAD)
-            if k >= 2:
-                store(k - 2, "add", 0, N_ADD)
-            if here:
-                horizontal(k, 0)
-            finish(0)
-            if here:
-                turn_add(k, 1)
-                haar_mm(k, 0)
-                turn_mm(k, 1)
-                horizontal(k, 1)
-            finish(2)
-            if here:
-                turn_add(k, 2)
-                haar_mm(k, 1)
-                turn_mm(k, 2)
-                horizontal(k, 2)
-            finish(4)
-            if behind:
-                store(k - 1, "mm", 0, N_MM)
-            if here:
-                turn_add(k, 3)
-                haar_mm(k, 2)
-                horizontal(k, 3)
-                quantise_t(k, "mm", 0, 2)
-                quantise_t(k, "mm", 2, 3)
-            else:
-                store(k - 1, "add", 0, 3)
-            finish(6)
-            if here:
-                turn_add(k, 4)
-                gather_blocks(k + 1)
-                horizontal(k, 4)
-                quantise_t(k, "add", 0, 4)
-                quantise_t(k, "add", 4, 5)
-            else:
-                store(k - 1, "add", 3, N_ADD)
+        A, M, F = 12, 20, 15
+        pair_of = {}
+        for way, pairs in (("add", ADD_PAIRS), ("mm", MM_PAIRS)):
+            for i, block in enumerate(pairs):
+                pair_of[block] = (way, i)
+        once = [
+            (-60, make_haar),
+            (-48, lambda: sort_w("add")),
+            (-4, lambda: turn_w("add", 0)),
+            (-2, lambda: turn_w("add", 1)),
+            (0, lambda: turn_w("add", 2)),
+            (2, lambda: turn_w("add", 3)),
+            (6, lambda: quantise_w("add")),
+            (-30, lambda: sort_w("mm")),
+            (20, lambda: turn_w("mm", 0)),
+            (24, lambda: turn_w("mm", 1)),
+            (28, lambda: turn_w("mm", 2)),
+            (32, lambda: turn_w("mm", 3)),
+            (44, lambda: quantise_w("mm")),
+        ]
+        stages = [
+            stage(-50, PAIR * A, N_ADD // PAIR, lambda i: vertical(i, nc.vector if i < 2 else nc.gpsimd)),
+            stage(-5, A, N_ADD, lambda n: turn_add(n, 0)),
+            stage(-14, A, N_ADD, lambda n: turn_add(n, 1)),
+            stage(-9, A, N_ADD, halve_odd),
+            stage(0, A, N_ADD, horizontal),
+            stage(6, M, N_MM, turn_mm),
+            stage(12, M, N_MM, copy_turned),
+            stage(19, M, N_MM, haar_mm),
+            stage(25, M, N_MM, copy_haar),
+            stage(-6, M, N_MM, gather_blocks),
+            stage(26, F, PAIRS, lambda s: quantise_t(*pair_of[s])),
+            stage(38, F, PAIRS, lambda s: multiply(*pair_of[s])),
+            stage(43, F, PAIRS, lambda s: add_bias(*pair_of[s])),
+            stage(52, F, PAIRS, lambda s: store(*pair_of[s])),
+            stage(-48, PAIR * A, N_ADD // PAIR - 4, lambda i: load("add", i + 4)),
+            stage(-20, PAIR * M, N_MM // PAIR - 2, lambda i: load("mm", i + 2)),
+        ]
+        first = min([s[0] for s in stages] + [when for when, do in once])
+        last = max(s[0] + s[1] * (s[2] - 1) for s in stages)
+        for tick in range(first, last + 1):
+            for start, step, count, do in stages:
+                n, rest = divmod(tick - start, step)
+                if rest == 0 and 0 <= n < count:
+                    do(n)
+            for when, do in once:
+                if when == tick:
+                    do()

@@ -24,52 +24,81 @@ PAIRS = 8192 // (PAIR * P)
 PERIOD = 8
 MM_PLACES = (2, 4, 7)
 
-ADD_PAIRS = [b for b in range(PAIRS) if b % PERIOD not in MM_PLACES]
-MM_PAIRS = [b for b in range(PAIRS) if b % PERIOD in MM_PLACES]
-N_ADD = PAIR * len(ADD_PAIRS)
-N_MM = PAIR * len(MM_PAIRS)
-ADD_STEP = 3
-MM_STEP = 5
-MM_START = 6
+ADD_PAIRS = [s for s in range(PAIRS) if s % PERIOD not in MM_PLACES]
+MM_PAIRS = [s for s in range(PAIRS) if s % PERIOD in MM_PLACES]
+N_ADD = PAIR * len(ADD_PAIRS) - 1
+N_MM = PAIR * len(MM_PAIRS) + 1
+ADD_GROUPS = [2] * 19 + [1]
+RUN = 1
 
 
 def tile_waveletlinearlayer_t_kernel(tc, x, W, b, out):
     nc = tc.nc
     with ExitStack() as ctx:
-        const = ctx.enter_context(tc.tile_pool(name="const", bufs=1))
-        x_pool = ctx.enter_context(tc.tile_pool(name="x_pool", bufs=6))
-        vert_pool = ctx.enter_context(tc.tile_pool(name="vert_pool", bufs=6))
-        ring = ctx.enter_context(tc.tile_pool(name="ring", bufs=3))
-        psum_single = ctx.enter_context(tc.psum_pool(name="psum_single", bufs=1))
-        psum_ring = ctx.enter_context(tc.psum_pool(name="psum_ring", bufs=2))
+        def sbuf(name, bufs):
+            return ctx.enter_context(tc.tile_pool(name=name, bufs=bufs))
+
+        def psum(name, bufs):
+            return ctx.enter_context(tc.psum_pool(name=name, bufs=bufs))
+
+        const = sbuf("const", 1)
+        x_pool = sbuf("x_pool", 6)
+        x_mm_pool = sbuf("x_mm_pool", 6)
+        vert_pool = sbuf("vert_pool", 6)
+        ring = sbuf("ring", 3)
+        grouped_pool = sbuf("grouped_pool", 6)
+        codes_pool = sbuf("codes_pool", 6)
+        result_pool = sbuf("result_pool", 6)
+        psum_single = psum("psum_single", 1)
+        psum_ring = psum("psum_ring", 2)
+        psum_acc = psum("psum_acc", 2)
         ctx.enter_context(tc.manual_schedule())
 
         live = {}
+        tiles_of = {}
+        for way, pairs in (("add", ADD_PAIRS), ("mm", MM_PAIRS)):
+            for i, s in enumerate(pairs):
+                tiles_of[s] = [(way, PAIR * i), (way, PAIR * i + 1)]
+        tiles_of[ADD_PAIRS[-1]] = tiles_of[MM_PAIRS[-1]]
+        tiles_of[MM_PAIRS[-1]] = [("add", N_ADD - 1), ("mm", N_MM - 1)]
+        where = {tile: (s, r) for s in range(PAIRS) for r, tile in enumerate(tiles_of[s])}
+        place = {}
+        sizes = {"add": ADD_GROUPS, "mm": [PAIR] * len(MM_PAIRS) + [1]}
+        first_row = {}
+        row = 0
+        for way in ("add", "mm"):
+            n = 0
+            for i, size in enumerate(sizes[way]):
+                first_row[way, i] = row
+                row += size * P
+                for r in range(size):
+                    place[way, n] = (i, r)
+                    n += 1
 
-        def pair_rows(ap, way, i):
-            block = (ADD_PAIRS if way == "add" else MM_PAIRS)[i]
-            rows = PAIR * P
-            return ap[block * rows : (block + 1) * rows, :].rearrange("(p r) f -> p r f", r=PAIR)
+        def group_rows(ap, way, i):
+            size = sizes[way][i]
+            return ap[first_row[way, i] : first_row[way, i] + size * P, :].rearrange(
+                "(p r) f -> p r f", r=size
+            )
 
         def load(way, i):
-            tile = x_pool.tile([P, PAIR * FEAT], BF16, tag="x_" + way, name="x_pair")
+            pool = x_pool if way == "add" else x_mm_pool
+            tile = pool.tile([P, max(sizes[way]) * FEAT], BF16, name="x_rows")
             live["x", way, i] = tile
             nc.sync.dma_start(
-                out=tile[:].rearrange("p (r f) -> p r f", f=FEAT), in_=pair_rows(x, way, i)
+                out=tile[:, : sizes[way][i] * FEAT].rearrange("p (r f) -> p r f", f=FEAT),
+                in_=group_rows(x, way, i),
             )
-
-        def x_tile(way, n):
-            r = n % PAIR
-            return live["x", way, n // PAIR][:, r * FEAT : (r + 1) * FEAT]
 
         def vertical(i, engine):
-            vert = vert_pool.tile([P, PAIR * FEAT], F32, name="vert")
+            size = ADD_GROUPS[i]
+            vert = vert_pool.tile([P, max(ADD_GROUPS) * FEAT], F32, name="vert")
             live["vert", i] = vert
-            vert_view = vert[:].rearrange(
-                "p (r e t v q j) -> p e v t r q j", r=PAIR, e=2, t=4, v=2, q=8, j=8
+            vert_view = vert[:, : size * FEAT].rearrange(
+                "p (r e t v q j) -> p e v t r q j", r=size, e=2, t=4, v=2, q=8, j=8
             )
-            x_view = live["x", "add", i][:].rearrange(
-                "p (r q t s j e) -> p s e t r q j", r=PAIR, q=8, t=4, s=2, j=8, e=2
+            x_view = live["x", "add", i][:, : size * FEAT].rearrange(
+                "p (r q t s j e) -> p s e t r q j", r=size, q=8, t=4, s=2, j=8, e=2
             )
             for e in (1, 0):
                 for v in range(2):
@@ -81,17 +110,14 @@ def tile_waveletlinearlayer_t_kernel(tc, x, W, b, out):
                     )
 
         def turn_add(n, e):
-            if e == 1:
-                bank = psum_single.tile([P, BANK], F32, name="odd")
-            else:
-                bank = psum_ring.tile([P, BANK], F32, name="even")
+            pool, name = (psum_single, "odd") if e == 1 else (psum_ring, "even")
+            bank = pool.tile([P, BANK], F32, tag=name, name="bank")
             live["bank", n, e] = bank
+            i, r = place["add", n]
             for t in range(SLOTS):
-                c0 = (n % PAIR) * FEAT + (e * SLOTS + t) * P
+                c0 = r * FEAT + (e * SLOTS + t) * P
                 nc.tensor.transpose(
-                    bank[:, t * P : (t + 1) * P],
-                    live["vert", n // PAIR][:, c0 : c0 + P],
-                    ident_f32[:],
+                    bank[:, t * P : (t + 1) * P], live["vert", i][:, c0 : c0 + P], ident_f32[:]
                 )
 
         def halve_odd(n):
@@ -104,21 +130,23 @@ def tile_waveletlinearlayer_t_kernel(tc, x, W, b, out):
                 scale=0.5,
             )
 
-        def grouped_view(way, n, g):
-            r = n % PAIR
-            if r == 0 and g == 0:
-                live["grouped", way, n // PAIR] = ring.tile(
-                    [P, PAIR * PASSES * BANK], BF16, align_bytes=64, tag="grouped_" + way, name="grouped"
+        def grouped_tile(way, n):
+            s, r = where[way, n]
+            run = s // RUN
+            if ("grouped", run) not in live:
+                live["grouped", run] = grouped_pool.tile(
+                    [P, RUN * PAIR * PASSES * BANK], BF16, align_bytes=64, name="grouped"
                 )
-            c0 = (r * PASSES + g) * BANK
-            return live["grouped", way, n // PAIR][:, c0 : c0 + BANK].rearrange(
-                "p (n t) -> p n t", t=SLOTS
-            )
+            c0 = (s % RUN * PAIR + r) * PASSES * BANK
+            return live["grouped", run][:, c0 : c0 + PASSES * BANK]
 
         def horizontal(n):
+            grouped = grouped_tile("add", n)
             for h in range(PASSES):
                 nc.vector.scalar_tensor_tensor(
-                    out=grouped_view("add", n, h),
+                    out=grouped[:, h * BANK : (h + 1) * BANK].rearrange(
+                        "p (n t) -> p n t", t=SLOTS
+                    ),
                     in0=live["bank", n, 0][:].rearrange("p (t n) -> p n t", t=SLOTS),
                     scalar=0.5,
                     in1=live["odd_half", n][:],
@@ -129,9 +157,12 @@ def tile_waveletlinearlayer_t_kernel(tc, x, W, b, out):
         def gather_blocks(n):
             x_sorted = ring.tile([P, FEAT // 2], F32, name="x_sorted")
             live["x_sorted", n] = x_sorted
+            i, r = place["mm", n]
             nc.scalar.copy(
                 out=x_sorted[:].rearrange("p (t m w) -> p t m w", t=4, m=8, w=16),
-                in_=x_tile("mm", n).bitcast(F32).rearrange("p (m t w) -> p t m w", m=8, t=4, w=16),
+                in_=live["x", "mm", i][:, r * FEAT : (r + 1) * FEAT]
+                .bitcast(F32)
+                .rearrange("p (m t w) -> p t m w", m=8, t=4, w=16),
             )
 
         def eight_transposes(src, row_tiles, r, pool, tag):
@@ -149,10 +180,9 @@ def tile_waveletlinearlayer_t_kernel(tc, x, W, b, out):
             )
 
         def copy_turned(n):
-            bank = live["turned", n]
             x_turned = ring.tile([P, PASSES * SLOTS * P], BF16, name="x_turned")
             live["x_turned", n] = x_turned
-            nc.scalar.copy(out=x_turned[:], in_=bank[:])
+            nc.scalar.copy(out=x_turned[:], in_=live["turned", n][:])
 
         def haar_mm(n):
             for g in range(PASSES):
@@ -167,31 +197,32 @@ def tile_waveletlinearlayer_t_kernel(tc, x, W, b, out):
                 )
 
         def copy_haar(n):
+            grouped = grouped_tile("mm", n)
             for g in range(PASSES):
                 nc.scalar.copy(
-                    out=grouped_view("mm", n, g),
+                    out=grouped[:, g * BANK : (g + 1) * BANK].rearrange(
+                        "p (n t) -> p n t", t=SLOTS
+                    ),
                     in_=live["haar_out", n, g][:].rearrange("p (t n) -> p n t", t=SLOTS),
                 )
 
-        def quantise(values, words, name, pool):
-            codes = pool.tile([P, words], U32, align_bytes=64, tag="codes_" + name, name="codes")
-            scales = pool.tile([P, words], U8, align_bytes=64, tag="scales_" + name, name="scales")
-            nc.vector.quantize_mx(out=codes[:].bitcast(FP8X4), scales=scales[:], in_=values)
-            return codes, scales
-
-        def quantise_t(way, i):
-            live["t", way, i] = quantise(
-                live["grouped", way, i][:], PAIR * PASSES * P, way, ring
+        def quantise_run(j):
+            words = RUN * PAIR * PASSES * P
+            codes = codes_pool.tile([P, words], U32, align_bytes=64, name="codes")
+            scales = codes_pool.tile([P, words], U8, align_bytes=64, name="scales")
+            live["t", j] = (codes, scales)
+            nc.vector.quantize_mx(
+                out=codes[:].bitcast(FP8X4), scales=scales[:], in_=live["grouped", j][:]
             )
 
-        def multiply(way, i):
-            codes, scales = live["t", way, i]
-            w_codes, w_scales = w_mx[way]
+        def multiply(s):
+            codes, scales = live["t", s // RUN]
             for r in range(PAIR):
-                acc = psum_ring.tile([P, OUT], F32, name="acc")
-                live["acc", way, i, r] = acc
+                w_codes, w_scales = w_mx[tiles_of[s][r][0]]
+                acc = psum_acc.tile([P, OUT], F32, name="acc")
+                live["acc", s, r] = acc
                 for g in range(PASSES):
-                    c0 = (r * PASSES + g) * P
+                    c0 = ((s % RUN * PAIR + r) * PASSES + g) * P
                     nc.tensor.matmul_mx(
                         out=acc[:],
                         lhsT=codes[:, c0 : c0 + P].bitcast(FP8X4),
@@ -202,16 +233,23 @@ def tile_waveletlinearlayer_t_kernel(tc, x, W, b, out):
                         stop=(g == PASSES - 1),
                     )
 
-        def add_bias(way, i):
-            result = ring.tile([P, PAIR, OUT], F32, tag="result_" + way, align_bytes=64, name="result")
-            live["result", way, i] = result
+        def add_bias(s):
+            result = result_pool.tile([P, PAIR, OUT], F32, align_bytes=64, name="result")
+            live["result", s] = result
             for r in range(PAIR):
                 nc.vector.tensor_tensor(
-                    out=result[:, r, :], in0=live["acc", way, i, r][:], in1=bias[:], op=ALU.add
+                    out=result[:, r, :], in0=live["acc", s, r][:], in1=bias[:], op=ALU.add
                 )
 
-        def store(way, i):
-            nc.sync.dma_start(out=pair_rows(out, way, i), in_=live["result", way, i][:])
+        def store(s):
+            result = live["result", s]
+            (way0, n0), (way1, n1) = tiles_of[s]
+            (g0, r0), (g1, r1) = place[way0, n0], place[way1, n1]
+            if (way0, g0) == (way1, g1):
+                nc.sync.dma_start(out=group_rows(out, way0, g0)[:, r0 : r1 + 1, :], in_=result[:])
+            else:
+                nc.sync.dma_start(out=group_rows(out, way0, g0)[:, r0, :], in_=result[:, 0, :])
+                nc.sync.dma_start(out=group_rows(out, way1, g1)[:, r1, :], in_=result[:, 1, :])
 
         def sort_w(way):
             w_sorted[way] = const.tile([P, 2 * FEAT], F32, name="w_sorted_" + way)
@@ -237,7 +275,7 @@ def tile_waveletlinearlayer_t_kernel(tc, x, W, b, out):
                 w_grouped[way] = const.tile(
                     [P, PASSES * SLOTS * OUT], BF16, align_bytes=64, name="w_grouped_" + way
                 )
-            bank = eight_transposes(w_sorted[way][:].bitcast(BF16), 4, o, psum_ring, "acc")
+            bank = eight_transposes(w_sorted[way][:].bitcast(BF16), 4, o, psum_acc, "acc")
             dst = w_grouped[way][:].rearrange("p (g m t) -> p g m t", g=PASSES, t=SLOTS)[
                 :, :, o * P : (o + 1) * P
             ]
@@ -248,7 +286,12 @@ def tile_waveletlinearlayer_t_kernel(tc, x, W, b, out):
                 nc.scalar.copy(out=dst, in_=src)
 
         def quantise_w(way):
-            w_mx[way] = quantise(w_grouped[way][:], PASSES * OUT, "w_" + way, const)
+            codes = const.tile([P, PASSES * OUT], U32, align_bytes=64, name="w_codes_" + way)
+            scales = const.tile([P, PASSES * OUT], U8, align_bytes=64, name="w_scales_" + way)
+            w_mx[way] = (codes, scales)
+            nc.vector.quantize_mx(
+                out=codes[:].bitcast(FP8X4), scales=scales[:], in_=w_grouped[way][:]
+            )
 
         w_rows = const.tile([P, 4 * FEAT], BF16)
         bias = const.tile([P, OUT], BF16)
@@ -273,17 +316,12 @@ def tile_waveletlinearlayer_t_kernel(tc, x, W, b, out):
             stage1 = const.tile([P, P], F32, name="stage1")
             i_view = ident[:].rearrange("p (d y s l) -> p s d y l", d=2, y=2, s=2, l=16)
             s_view = stage1[:].rearrange("p (d v y l) -> p v d y l", d=2, v=2, y=2, l=16)
-            nc.vector.tensor_tensor(out=s_view[:, 0], in0=i_view[:, 0], in1=i_view[:, 1], op=ALU.add)
-            nc.vector.tensor_tensor(
-                out=s_view[:, 1], in0=i_view[:, 0], in1=i_view[:, 1], op=ALU.subtract
-            )
             stage2 = const.tile([P, P], F32, name="stage2")
             e_view = stage1[:].rearrange("p (d m e) -> p e d m", m=32, e=2)
             h_view = stage2[:].rearrange("p (d h m) -> p h d m", h=2, m=32)
-            nc.vector.tensor_tensor(out=h_view[:, 0], in0=e_view[:, 0], in1=e_view[:, 1], op=ALU.add)
-            nc.vector.tensor_tensor(
-                out=h_view[:, 1], in0=e_view[:, 0], in1=e_view[:, 1], op=ALU.subtract
-            )
+            for dst, src in ((s_view, i_view), (h_view, e_view)):
+                for k, op in enumerate((ALU.add, ALU.subtract)):
+                    nc.vector.tensor_tensor(out=dst[:, k], in0=src[:, 0], in1=src[:, 1], op=op)
             nc.vector.tensor_scalar_mul(out=haar[:], in0=stage2[:], scalar1=0.5)
 
         haar = const.tile([P, P], BF16)
@@ -291,15 +329,15 @@ def tile_waveletlinearlayer_t_kernel(tc, x, W, b, out):
         w_grouped = {}
         w_mx = {}
 
-        def stage(start, step, count, do):
-            return (start, step, count, do)
+        A, M, F, M0 = 12, 19, 15, 20
 
-        A, M, F = 12, 20, 15
-        pair_of = {}
-        for way, pairs in (("add", ADD_PAIRS), ("mm", MM_PAIRS)):
-            for i, block in enumerate(pairs):
-                pair_of[block] = (way, i)
-        once = [
+        def stage(start, step, count, do):
+            return [(start + n * step, do, n) for n in range(count)]
+
+        def once(start, do):
+            return (start, lambda n: do(), 0)
+
+        works = [once(when, do) for when, do in [
             (-60, make_haar),
             (-48, lambda: sort_w("add")),
             (-4, lambda: turn_w("add", 0)),
@@ -313,32 +351,30 @@ def tile_waveletlinearlayer_t_kernel(tc, x, W, b, out):
             (28, lambda: turn_w("mm", 2)),
             (32, lambda: turn_w("mm", 3)),
             (44, lambda: quantise_w("mm")),
-        ]
-        stages = [
-            stage(-50, PAIR * A, N_ADD // PAIR, lambda i: vertical(i, nc.vector if i < 2 else nc.gpsimd)),
+        ]]
+        first_tile = [sum(ADD_GROUPS[:i]) for i in range(len(ADD_GROUPS))]
+        work = [
+            [(-50 + A * n, lambda i: vertical(i, nc.vector if i < 2 else nc.gpsimd), i) for i, n in enumerate(first_tile)],
             stage(-5, A, N_ADD, lambda n: turn_add(n, 0)),
             stage(-14, A, N_ADD, lambda n: turn_add(n, 1)),
             stage(-9, A, N_ADD, halve_odd),
             stage(0, A, N_ADD, horizontal),
-            stage(6, M, N_MM, turn_mm),
-            stage(12, M, N_MM, copy_turned),
-            stage(19, M, N_MM, haar_mm),
-            stage(25, M, N_MM, copy_haar),
-            stage(-6, M, N_MM, gather_blocks),
-            stage(26, F, PAIRS, lambda s: quantise_t(*pair_of[s])),
-            stage(38, F, PAIRS, lambda s: multiply(*pair_of[s])),
-            stage(43, F, PAIRS, lambda s: add_bias(*pair_of[s])),
-            stage(52, F, PAIRS, lambda s: store(*pair_of[s])),
-            stage(-48, PAIR * A, N_ADD // PAIR - 4, lambda i: load("add", i + 4)),
-            stage(-20, PAIR * M, N_MM // PAIR - 2, lambda i: load("mm", i + 2)),
+            stage(M0 + -14, M, N_MM, turn_mm),
+            stage(M0 + -8, M, N_MM, copy_turned),
+            stage(M0 + -1, M, N_MM, haar_mm),
+            stage(M0 + 5, M, N_MM, copy_haar),
+            stage(M0 + -26, M, N_MM, gather_blocks),
+            stage(26, RUN * F, PAIRS // RUN, quantise_run),
+            stage(38, F, PAIRS, multiply),
+            stage(43, F, PAIRS, add_bias),
+            stage(52, F, PAIRS, store),
+            [(-144 + A * n, lambda i: load("add", i), i) for i, n in enumerate(first_tile)][4:],
+            stage(M0 - 40, PAIR * M, len(MM_PAIRS) - 1, lambda i: load("mm", i + 2)),
+            works,
         ]
-        first = min([s[0] for s in stages] + [when for when, do in once])
-        last = max(s[0] + s[1] * (s[2] - 1) for s in stages)
-        for tick in range(first, last + 1):
-            for start, step, count, do in stages:
-                n, rest = divmod(tick - start, step)
-                if rest == 0 and 0 <= n < count:
-                    do(n)
-            for when, do in once:
-                if when == tick:
-                    do()
+        ticks = [w[0] for part in work for w in part]
+        for tick in range(min(ticks), max(ticks) + 1):
+            for part in work:
+                for when, do, n in part:
+                    if when == tick:
+                        do(n)

@@ -215,9 +215,9 @@ def tile_waveletlinearlayer_t_kernel(tc, x, W, b, out):
                 out=codes[:].bitcast(FP8X4), scales=scales[:], in_=live["grouped", j][:]
             )
 
-        def multiply(s):
+        def multiply(s, tiles):
             codes, scales = live["t", s // RUN]
-            for r in range(PAIR):
+            for r in tiles:
                 w_codes, w_scales = w_mx[tiles_of[s][r][0]]
                 acc = psum_acc.tile([P, OUT], F32, name="acc")
                 live["acc", s, r] = acc
@@ -233,10 +233,13 @@ def tile_waveletlinearlayer_t_kernel(tc, x, W, b, out):
                         stop=(g == PASSES - 1),
                     )
 
-        def add_bias(s):
-            result = result_pool.tile([P, PAIR, OUT], F32, align_bytes=64, name="result")
-            live["result", s] = result
-            for r in range(PAIR):
+        def add_bias(s, tiles):
+            if 0 in tiles:
+                live["result", s] = result_pool.tile(
+                    [P, PAIR, OUT], F32, align_bytes=64, name="result"
+                )
+            result = live["result", s]
+            for r in tiles:
                 nc.vector.tensor_tensor(
                     out=result[:, r, :], in0=live["acc", s, r][:], in1=bias[:], op=ALU.add
                 )
@@ -365,9 +368,11 @@ def tile_waveletlinearlayer_t_kernel(tc, x, W, b, out):
             stage(M0 + 5, M, N_MM, copy_haar),
             stage(M0 + -26, M, N_MM, gather_blocks),
             stage(26, RUN * F, PAIRS // RUN, quantise_run),
-            stage(38, F, PAIRS, multiply),
-            stage(43, F, PAIRS, add_bias),
-            stage(52, F, PAIRS, store),
+            stage(36, F, PAIRS, lambda s: multiply(s, (0,))),
+            stage(43, F, PAIRS, lambda s: multiply(s, (1,))),
+            stage(41, F, PAIRS, lambda s: add_bias(s, (0,))),
+            stage(48, F, PAIRS, lambda s: add_bias(s, (1,))),
+            stage(57, F, PAIRS, store),
             [(-144 + A * n, lambda i: load("add", i), i) for i, n in enumerate(first_tile)][4:],
             stage(M0 - 40, PAIR * M, len(MM_PAIRS) - 1, lambda i: load("mm", i + 2)),
             works,

@@ -51,7 +51,7 @@ def tile_waveletlinearlayer_t_kernel(tc, x, W, b, out):
         result_pool = sbuf("result_pool", 6)
         psum_single = psum("psum_single", 1)
         psum_ring = psum("psum_ring", 2)
-        psum_acc = psum("psum_acc", 2)
+        psum_acc = psum("psum_acc", 3)
         ctx.enter_context(tc.manual_schedule())
 
         live = {}
@@ -185,11 +185,11 @@ def tile_waveletlinearlayer_t_kernel(tc, x, W, b, out):
             nc.scalar.copy(out=x_turned[:], in_=live["turned", n][:])
 
         def haar_mm(n):
+            bank = psum_single.tile([P, PASSES * BANK], BF16, name="haar_out")
+            live["haar_out", n] = bank
             for g in range(PASSES):
-                bank = psum_ring.tile([P, BANK], F32, name="haar_out")
-                live["haar_out", n, g] = bank
                 nc.tensor.matmul(
-                    out=bank[:],
+                    out=bank[:, g * BANK : (g + 1) * BANK],
                     lhsT=haar[:],
                     rhs=live["x_turned", n][:, g * BANK : (g + 1) * BANK],
                     start=True,
@@ -197,14 +197,10 @@ def tile_waveletlinearlayer_t_kernel(tc, x, W, b, out):
                 )
 
         def copy_haar(n):
-            grouped = grouped_tile("mm", n)
-            for g in range(PASSES):
-                nc.scalar.copy(
-                    out=grouped[:, g * BANK : (g + 1) * BANK].rearrange(
-                        "p (n t) -> p n t", t=SLOTS
-                    ),
-                    in_=live["haar_out", n, g][:].rearrange("p (t n) -> p n t", t=SLOTS),
-                )
+            nc.scalar.copy(
+                out=grouped_tile("mm", n).rearrange("p (g n t) -> p g n t", g=PASSES, t=SLOTS),
+                in_=live["haar_out", n][:].rearrange("p (g t n) -> p g n t", g=PASSES, t=SLOTS),
+            )
 
         def quantise_run(j):
             words = RUN * PAIR * PASSES * P

@@ -354,9 +354,9 @@ def tile_waveletlinearlayer_t_kernel(tc, x, W, b, out):
         first_tile = [sum(ADD_GROUPS[:i]) for i in range(len(ADD_GROUPS))]
         work = [
             [(-50 + A * n, lambda i: vertical(i, nc.vector if i < 2 else nc.gpsimd), i) for i, n in enumerate(first_tile)],
-            stage(-5, A, N_ADD, lambda n: turn_add(n, 0)),
-            stage(-14, A, N_ADD, lambda n: turn_add(n, 1)),
-            stage(-9, A, N_ADD, halve_odd),
+            stage(-6, A, N_ADD, lambda n: turn_add(n, 0)),
+            stage(-15, A, N_ADD, lambda n: turn_add(n, 1)),
+            stage(-10, A, N_ADD, halve_odd),
             stage(0, A, N_ADD, horizontal),
             stage(M0 + -14, M, N_MM, turn_mm),
             stage(M0 + -8, M, N_MM, copy_turned),
@@ -364,10 +364,10 @@ def tile_waveletlinearlayer_t_kernel(tc, x, W, b, out):
             stage(M0 + 5, M, N_MM, copy_haar),
             stage(M0 + -26, M, N_MM, gather_blocks),
             stage(26, RUN * F, PAIRS // RUN, quantise_run),
-            stage(36, F, PAIRS, lambda s: multiply(s, (0,))),
-            stage(43, F, PAIRS, lambda s: multiply(s, (1,))),
-            stage(41, F, PAIRS, lambda s: add_bias(s, (0,))),
-            stage(48, F, PAIRS, lambda s: add_bias(s, (1,))),
+            stage(40, F, PAIRS, lambda s: multiply(s, (0,))),
+            stage(47, F, PAIRS, lambda s: multiply(s, (1,))),
+            stage(45, F, PAIRS, lambda s: add_bias(s, (0,))),
+            stage(52, F, PAIRS, lambda s: add_bias(s, (1,))),
             stage(57, F, PAIRS, store),
             [(-144 + A * n, lambda i: load("add", i), i) for i, n in enumerate(first_tile)][4:],
             stage(M0 - 40, PAIR * M, len(MM_PAIRS) - 1, lambda i: load("mm", i + 2)),

from contextlib import ExitStack

import concourse.mybir as mybir
from concourse.masks import make_identity

FP8X4 = mybir.dt.float8_e4m3fn_x4
BF16 = mybir.dt.bfloat16
F32 = mybir.dt.float32
U32 = mybir.dt.uint32
U8 = mybir.dt.uint8
ALU = mybir.AluOpType
ACT = mybir.ActivationFunctionType

FLOPS = 2 * 8192 * 1024 * 512

P = 128
FEAT = 1024
OUT = 512
SLOTS = 4
PASSES = 2
BANK = 512
PAIR = 2
PAIRS = 8192 // (PAIR * P)
PERIOD = 8
MM_PLACES = (2, 4, 7)

ADD_PAIRS = [s for s in range(PAIRS) if s % PERIOD not in MM_PLACES]
MM_PAIRS = [s for s in range(PAIRS) if s % PERIOD in MM_PLACES]
N_ADD = PAIR * len(ADD_PAIRS) - 1
N_MM = PAIR * len(MM_PAIRS) + 1
ADD_GROUPS = [2] * 19 + [1]
RUN = 1


def tile_waveletlinearlayer_t_kernel(tc, x, W, b, out):
    nc = tc.nc
    with ExitStack() as ctx:
        def sbuf(name, bufs):
            return ctx.enter_context(tc.tile_pool(name=name, bufs=bufs))

        def psum(name, bufs):
            return ctx.enter_context(tc.psum_pool(name=name, bufs=bufs))

        const = sbuf("const", 1)
        x_pool = sbuf("x_pool", 6)
        x_mm_pool = sbuf("x_mm_pool", 6)
        vert_pool = sbuf("vert_pool", 6)
        ring = sbuf("ring", 3)
        grouped_pool = sbuf("grouped_pool", 6)
        codes_pool = sbuf("codes_pool", 6)
        result_pool = sbuf("result_pool", 6)
        psum_single = psum("psum_single", 1)
        psum_ring = psum("psum_ring", 2)
        psum_acc = psum("psum_acc", 3)
        ctx.enter_context(tc.manual_schedule())

        live = {}
        tiles_of = {}
        for way, pairs in (("add", ADD_PAIRS), ("mm", MM_PAIRS)):
            for i, s in enumerate(pairs):
                tiles_of[s] = [(way, PAIR * i), (way, PAIR * i + 1)]
        tiles_of[ADD_PAIRS[-1]] = tiles_of[MM_PAIRS[-1]]
        tiles_of[MM_PAIRS[-1]] = [("add", N_ADD - 1), ("mm", N_MM - 1)]
        where = {tile: (s, r) for s in range(PAIRS) for r, tile in enumerate(tiles_of[s])}
        place = {}
        sizes = {"add": ADD_GROUPS, "mm": [PAIR] * len(MM_PAIRS) + [1]}
        first_row = {}
        row = 0
        for way in ("add", "mm"):
            n = 0
            for i, size in enumerate(sizes[way]):
                first_row[way, i] = row
                row += size * P
                for r in range(size):
                    place[way, n] = (i, r)
                    n += 1

        def group_rows(ap, way, i):
            size = sizes[way][i]
            return ap[first_row[way, i] : first_row[way, i] + size * P, :].rearrange(
                "(p r) f -> p r f", r=size
            )

        def load(way, i):
            pool = x_pool if way == "add" else x_mm_pool
            tile = pool.tile([P, max(sizes[way]) * FEAT], BF16, name="x_rows")
            live["x", way, i] = tile
            nc.sync.dma_start(
                out=tile[:, : sizes[way][i] * FEAT].rearrange("p (r f) -> p r f", f=FEAT),
                in_=group_rows(x, way, i),
            )

        def vertical(i, engine):
            size = ADD_GROUPS[i]
            vert = vert_pool.tile([P, max(ADD_GROUPS) * FEAT], F32, name="vert")
            live["vert", i] = vert
            vert_view = vert[:, : size * FEAT].rearrange(
                "p (r e t v q j) -> p e v t r q j", r=size, e=2, t=4, v=2, q=8, j=8
            )
            x_view = live["x", "add", i][:, : size * FEAT].rearrange(
                "p (r q t s j e) -> p s e t r q j", r=size, q=8, t=4, s=2, j=8, e=2
            )
            for e in (1, 0):
                for v in range(2):
                    engine.tensor_tensor(
                        out=vert_view[:, e, v],
                        in0=x_view[:, 0, e],
                        in1=x_view[:, 1, e],
                        op=(ALU.add if v == 0 else ALU.subtract),
                    )

        def turn_add(n, e):
            pool, name = (psum_single, "odd") if e == 1 else (psum_ring, "even")
            bank = pool.tile([P, BANK], F32, tag=name, name="bank")
            live["bank", n, e] = bank
            i, r = place["add", n]
            for t in range(SLOTS):
                c0 = r * FEAT + (e * SLOTS + t) * P
                nc.tensor.transpose(
                    bank[:, t * P : (t + 1) * P], live["vert", i][:, c0 : c0 + P], ident_f32[:]
                )

        def halve_odd(n):
            odd_half = ring.tile([P, P, SLOTS], F32, name="odd_half")
            live["odd_half", n] = odd_half
            nc.scalar.activation(
                out=odd_half[:],
                in_=live["bank", n, 1][:].rearrange("p (t n) -> p n t", t=SLOTS),
                func=ACT.Copy,
                scale=0.5,
            )

        def grouped_tile(way, n):
            s, r = where[way, n]
            run = s // RUN
            if ("grouped", run) not in live:
                live["grouped", run] = grouped_pool.tile(
                    [P, RUN * PAIR * PASSES * BANK], BF16, align_bytes=64, name="grouped"
                )
            c0 = (s % RUN * PAIR + r) * PASSES * BANK
            return live["grouped", run][:, c0 : c0 + PASSES * BANK]

        def horizontal(n):
            grouped = grouped_tile("add", n)
            for h in range(PASSES):
                nc.vector.scalar_tensor_tensor(
                    out=grouped[:, h * BANK : (h + 1) * BANK].rearrange(
                        "p (n t) -> p n t", t=SLOTS
                    ),
                    in0=live["bank", n, 0][:].rearrange("p (t n) -> p n t", t=SLOTS),
                    scalar=0.5,
                    in1=live["odd_half", n][:],
                    op0=ALU.mult,
                    op1=(ALU.add if h == 0 else ALU.subtract),
                )

        def gather_blocks(n):
            x_sorted = ring.tile([P, FEAT // 2], F32, name="x_sorted")
            live["x_sorted", n] = x_sorted
            i, r = place["mm", n]
            nc.scalar.copy(
                out=x_sorted[:].rearrange("p (t m w) -> p t m w", t=4, m=8, w=16),
                in_=live["x", "mm", i][:, r * FEAT : (r + 1) * FEAT]
                .bitcast(F32)
                .rearrange("p (m t w) -> p t m w", m=8, t=4, w=16),
            )

        def eight_transposes(src, row_tiles, r, pool, tag):
            bank = pool.tile([P, PASSES * SLOTS * P], BF16, tag=tag, name="turned")
            for g in range(PASSES):
                for t in range(SLOTS):
                    c0 = t * (row_tiles * PASSES * P) + r * PASSES * P + g * P
                    c1 = (g * SLOTS + t) * P
                    nc.tensor.transpose(bank[:, c1 : c1 + P], src[:, c0 : c0 + P], ident[:])
            return bank

        def turn_mm(n):
            live["turned", n] = eight_transposes(
                live["x_sorted", n][:].bitcast(BF16), 1, 0, psum_single, "turned"
            )

        def copy_turned(n):
            x_turned = ring.tile([P, PASSES * SLOTS * P], BF16, name="x_turned")
            live["x_turned", n] = x_turned
            nc.scalar.copy(out=x_turned[:], in_=live["turned", n][:])

        def haar_mm(n):
            bank = psum_single.tile([P, PASSES * BANK], BF16, name="haar_out")
            live["haar_out", n] = bank
            for g in range(PASSES):
                nc.tensor.matmul(
                    out=bank[:, g * BANK : (g + 1) * BANK],
                    lhsT=haar[:],
                    rhs=live["x_turned", n][:, g * BANK : (g + 1) * BANK],
                    start=True,
                    stop=True,
                )

        def copy_haar(n):
            nc.scalar.copy(
                out=grouped_tile("mm", n).rearrange("p (g n t) -> p g n t", g=PASSES, t=SLOTS),
                in_=live["haar_out", n][:].rearrange("p (g t n) -> p g n t", g=PASSES, t=SLOTS),
            )

        def quantise_run(j):
            words = RUN * PAIR * PASSES * P
            codes = codes_pool.tile([P, words], U32, align_bytes=64, name="codes")
            scales = codes_pool.tile([P, words], U8, align_bytes=64, name="scales")
            live["t", j] = (codes, scales)
            nc.vector.quantize_mx(
                out=codes[:].bitcast(FP8X4), scales=scales[:], in_=live["grouped", j][:]
            )

        def multiply(s, tiles):
            codes, scales = live["t", s // RUN]
            for r in tiles:
                w_codes, w_scales = w_mx[tiles_of[s][r][0]]
                acc = psum_acc.tile([P, OUT], F32, name="acc")
                live["acc", s, r] = acc
                for g in range(PASSES):
                    c0 = ((s % RUN * PAIR + r) * PASSES + g) * P
                    nc.tensor.matmul_mx(
                        out=acc[:],
                        lhsT=codes[:, c0 : c0 + P].bitcast(FP8X4),
                        lhsT_scale=scales[:, c0 : c0 + P],
                        rhs=w_codes[:, g * OUT : (g + 1) * OUT].bitcast(FP8X4),
                        rhs_scale=w_scales[:, g * OUT : (g + 1) * OUT],
                        start=(g == 0),
                        stop=(g == PASSES - 1),
                    )

        def add_bias(s, tiles):
            if 0 in tiles:
                live["result", s] = result_pool.tile(
                    [P, PAIR, OUT], F32, align_bytes=64, name="result"
                )
            result = live["result", s]
            for r in tiles:
                nc.vector.tensor_tensor(
                    out=result[:, r, :], in0=live["acc", s, r][:], in1=bias[:], op=ALU.add
                )

        def store(s):
            result = live["result", s]
            (way0, n0), (way1, n1) = tiles_of[s]
            (g0, r0), (g1, r1) = place[way0, n0], place[way1, n1]
            if (way0, g0) == (way1, g1):
                nc.sync.dma_start(out=group_rows(out, way0, g0)[:, r0 : r1 + 1, :], in_=result[:])
            else:
                nc.sync.dma_start(out=group_rows(out, way0, g0)[:, r0, :], in_=result[:, 0, :])
                nc.sync.dma_start(out=group_rows(out, way1, g1)[:, r1, :], in_=result[:, 1, :])

        def sort_w(way):
            w_sorted[way] = const.tile([P, 2 * FEAT], F32, name="w_sorted_" + way)
            words = w_rows[:].bitcast(F32)
            if way == "add":
                dst = w_sorted[way][:].rearrange(
                    "p (t o h v c y j) -> p t y o h v c j", t=4, o=4, h=2, v=2, c=4, y=2, j=4
                )
                src = words.rearrange(
                    "p (o c h v y t j) -> p t y o h v c j", o=4, c=4, h=2, v=2, y=2, t=4, j=4
                )
                for t in range(SLOTS):
                    for y in range(2):
                        nc.vector.tensor_copy(out=dst[:, t, y], in_=src[:, t, y])
            else:
                dst = w_sorted[way][:].rearrange("p (t o m j) -> p t o m j", t=4, o=4, m=32, j=4)
                src = words.rearrange("p (o m t j) -> p t o m j", o=4, m=32, t=4, j=4)
                for t in range(SLOTS):
                    nc.scalar.copy(out=dst[:, t], in_=src[:, t])

        def turn_w(way, o):
            if o == 0:
                w_grouped[way] = const.tile(
                    [P, PASSES * SLOTS * OUT], BF16, align_bytes=64, name="w_grouped_" + way
                )
            bank = eight_transposes(w_sorted[way][:].bitcast(BF16), 4, o, psum_acc, "acc")
            dst = w_grouped[way][:].rearrange("p (g m t) -> p g m t", g=PASSES, t=SLOTS)[
                :, :, o * P : (o + 1) * P
            ]
            src = bank[:].rearrange("p (g t n) -> p g n t", g=PASSES, t=SLOTS)
            if way == "add" and o % 2 == 0:
                nc.vector.tensor_copy(out=dst, in_=src)
            else:
                nc.scalar.copy(out=dst, in_=src)

        def quantise_w(way):
            codes = const.tile([P, PASSES * OUT], U32, align_bytes=64, name="w_codes_" + way)
            scales = const.tile([P, PASSES * OUT], U8, align_bytes=64, name="w_scales_" + way)
            w_mx[way] = (codes, scales)
            nc.vector.quantize_mx(
                out=codes[:].bitcast(FP8X4), scales=scales[:], in_=w_grouped[way][:]
            )

        w_rows = const.tile([P, 4 * FEAT], BF16)
        bias = const.tile([P, OUT], BF16)
        load("add", 0)
        nc.sync.dma_start(
            out=w_rows[:].rearrange("p (o f) -> p o f", f=FEAT),
            in_=W.rearrange("(o p) f -> p o f", p=P),
        )
        load("add", 1)
        load("mm", 0)
        load("add", 2)
        nc.sync.dma_start(out=bias[:], in_=b.partition_broadcast(P))
        load("mm", 1)
        load("add", 3)

        ident = const.tile([P, P], BF16)
        make_identity(nc, ident[:])
        ident_f32 = const.tile([P, P], F32)
        make_identity(nc, ident_f32[:])

        def make_haar():
            stage1 = const.tile([P, P], F32, name="stage1")
            i_view = ident[:].rearrange("p (d y s l) -> p s d y l", d=2, y=2, s=2, l=16)
            s_view = stage1[:].rearrange("p (d v y l) -> p v d y l", d=2, v=2, y=2, l=16)
            stage2 = const.tile([P, P], F32, name="stage2")
            e_view = stage1[:].rearrange("p (d m e) -> p e d m", m=32, e=2)
            h_view = stage2[:].rearrange("p (d h m) -> p h d m", h=2, m=32)
            for dst, src in ((s_view, i_view), (h_view, e_view)):
                for k, op in enumerate((ALU.add, ALU.subtract)):
                    nc.vector.tensor_tensor(out=dst[:, k], in0=src[:, 0], in1=src[:, 1], op=op)
            nc.vector.tensor_scalar_mul(out=haar[:], in0=stage2[:], scalar1=0.5)

        haar = const.tile([P, P], BF16)
        w_sorted = {}
        w_grouped = {}
        w_mx = {}

        A, M, F, M0 = 12, 19, 15, 20

        def stage(start, step, count, do):
            return [(start + n * step, do, n) for n in range(count)]

        def once(start, do):
            return (start, lambda n: do(), 0)

        works = [once(when, do) for when, do in [
            (-60, make_haar),
            (-48, lambda: sort_w("add")),
            (-4, lambda: turn_w("add", 0)),
            (-2, lambda: turn_w("add", 1)),
            (0, lambda: turn_w("add", 2)),
            (2, lambda: turn_w("add", 3)),
            (6, lambda: quantise_w("add")),
            (-30, lambda: sort_w("mm")),
            (20, lambda: turn_w("mm", 0)),
            (24, lambda: turn_w("mm", 1)),
            (28, lambda: turn_w("mm", 2)),
            (32, lambda: turn_w("mm", 3)),
            (44, lambda: quantise_w("mm")),
        ]]
        first_tile = [sum(ADD_GROUPS[:i]) for i in range(len(ADD_GROUPS))]
        work = [
            [(-50 + A * n, lambda i: vertical(i, nc.vector if i < 2 else nc.gpsimd), i) for i, n in enumerate(first_tile)],
            stage(-6, A, N_ADD, lambda n: turn_add(n, 0)),
            stage(-15, A, N_ADD, lambda n: turn_add(n, 1)),
            stage(-10, A, N_ADD, halve_odd),
            stage(0, A, N_ADD, horizontal),
            stage(M0 + -14, M, N_MM, turn_mm),
            stage(M0 + -8, M, N_MM, copy_turned),
            stage(M0 + -1, M, N_MM, haar_mm),
            stage(M0 + 5, M, N_MM, copy_haar),
            stage(M0 + -26, M, N_MM, gather_blocks),
            stage(26, RUN * F, PAIRS // RUN, quantise_run),
            stage(40, F, PAIRS, lambda s: multiply(s, (0,))),
            stage(47, F, PAIRS, lambda s: multiply(s, (1,))),
            stage(45, F, PAIRS, lambda s: add_bias(s, (0,))),
            stage(52, F, PAIRS, lambda s: add_bias(s, (1,))),
            stage(57, F, PAIRS, store),
            [(-144 + A * n, lambda i: load("add", i), i) for i, n in enumerate(first_tile)][4:],
            stage(M0 - 40, PAIR * M, len(MM_PAIRS) - 1, lambda i: load("mm", i + 2)),
            works,
        ]
        ticks = [w[0] for part in work for w in part]
        for tick in range(min(ticks), max(ticks) + 1):
            for part in work:
                for when, do, n in part:
                    if when == tick:
                        do(n)
